import numpy as np
import ml_dtypes


def mxq(x, axis, fmt="e4m3"):
    dtype, down = {"e4m3": (ml_dtypes.float8_e4m3fn, 7), "e5m2": (ml_dtypes.float8_e5m2, 14)}[fmt]
    v = np.moveaxis(np.asarray(x, np.float32).astype(ml_dtypes.bfloat16).astype(np.float64), axis, -1)
    blocks = v.reshape(v.shape[:-1] + (-1, 32))
    amax = np.abs(blocks).max(-1, keepdims=True)
    byte = np.maximum(np.where(amax > 0, np.frexp(amax)[1] - 1 + 127, 0) - down, 1)
    scale = np.exp2(byte - 127.0)
    codes = (blocks / scale).astype(np.float32).astype(dtype).astype(np.float64)
    return np.moveaxis((codes * scale).reshape(v.shape), -1, axis)


WIDE = False


def mx_kscale(k):
    if not WIDE:
        return np.ones(k)
    levels = np.array([10, -10, 5, -5, 0])
    a = np.random.permutation(np.resize(levels, k // 512 * 4)).reshape(k // 512, 4)
    idx = np.arange(k)
    return np.exp2(a[idx // 512, idx % 128 // 32])


BF16 = ml_dtypes.bfloat16


def bf(x):
    return np.asarray(x, np.float32).astype(BF16)


def f64(x):
    return np.asarray(x).astype(np.float64)


E2M1 = np.array([0.0, 0.5, 1.0, 1.5, 2.0, 3.0, 4.0, 6.0, -0.0, -0.5, -1.0, -1.5, -2.0, -3.0, -4.0, -6.0])


def pack_weight(w, fmt):
    k, n = w.shape
    w = f64(bf(w)).reshape(k // 32, 32, n)
    amax = np.abs(w).max(1)
    if fmt == "e4m3":
        byte = np.frexp(amax)[1] - 1 + 127 - 7
    else:
        mant, ex = np.frexp(amax / 6.0)
        byte = np.where(mant > 0.5, ex, ex - 1) + 127
    byte = np.clip(np.where(amax > 0, byte, 1), 1, 254)
    scaled = (w * np.exp2(127.0 - byte)[:, None, :]).reshape(k, n).astype(np.float32)
    by_word = np.ascontiguousarray(scaled.reshape(k // 512, 128, 4, n).transpose(0, 1, 3, 2))
    if fmt == "e4m3":
        words = by_word.astype(ml_dtypes.float8_e4m3fn).view(np.uint8)
    else:
        c = by_word.astype(ml_dtypes.float4_e2m1fn).view(np.uint8) & 0xF
        words = c[..., 0::2] | (c[..., 1::2] << 4)
    return np.ascontiguousarray(words), np.ascontiguousarray(byte.astype(np.uint8).reshape(k // 512, 16, n))


def unpack_weight(words, scales, fmt):
    g, p, n, _ = words.shape
    if fmt == "e4m3":
        vals = np.ascontiguousarray(words).view(ml_dtypes.float8_e4m3fn).astype(np.float64)
    else:
        nib = np.empty((g, p, n, 4), np.uint8)
        nib[..., 0::2] = words & 0xF
        nib[..., 1::2] = words >> 4
        vals = E2M1[nib]
    vals = vals * np.repeat(np.exp2(scales.astype(np.float64) - 127.0), 8, axis=1)[..., None]
    return vals.transpose(0, 1, 3, 2).reshape(g * 512, n)


B, M, N, P = 6, 1024, 1024, 512
EPS = 1e-05
FMT = "e4m3"


def normalize(v, axes, gamma, beta):
    mean = v.mean(axis=axes, keepdims=True)
    std = np.sqrt(v.var(axis=axes, keepdims=True, ddof=1))
    return gamma * ((v - mean) / (std + EPS)) + beta


def setup_inputs():
    s = mx_kscale(N)
    x = bf(np.random.standard_normal((B, M, N)) * s)
    xj_words, xj_scales = pack_weight(np.random.standard_normal((N, P)) * 0.5 / np.sqrt(N) / s[:, None], FMT)
    xi_words, xi_scales = pack_weight(np.random.standard_normal((M, P)) * 2.0 / np.sqrt(M), FMT)
    return {"x": x,
            "original_xj_y_words": xj_words,
            "original_xj_y_scales": xj_scales,
            "original_xi_y_words": xi_words,
            "original_xi_y_scales": xi_scales,
            "gamma_o_sum": bf(1.0 + 0.1 * np.random.standard_normal(P)),
            "gamma_o": bf(1.0 + 0.1 * np.random.standard_normal((P, P))),
            "beta_o_sum": bf(0.1 * np.random.standard_normal(P)),
            "beta_o": bf(0.1 * np.random.standard_normal((P, P)))}


def reference(x, original_xj_y_words, original_xj_y_scales, original_xi_y_words, original_xi_y_scales, gamma_o_sum, gamma_o, beta_o_sum, beta_o):
    oyy = mxq(f64(x), 2, "e4m3") @ unpack_weight(original_xj_y_words, original_xj_y_scales, FMT)
    o_sum = normalize(oyy.sum(axis=-2), (-1,), f64(gamma_o_sum), f64(beta_o_sum)) + 1.0
    oyy = mxq(np.swapaxes(oyy, -1, -2), 2, "e4m3") @ unpack_weight(original_xi_y_words, original_xi_y_scales, FMT)
    oyy = np.swapaxes(oyy, -1, -2)
    oyy = normalize(oyy, (-2, -1), f64(gamma_o), f64(beta_o))
    return oyy, o_sum

@@ -1,0 +1,362 @@
+from contextlib import ExitStack
+
+import concourse.mybir as mybir
+from concourse.masks import make_identity
+
+F32 = mybir.dt.float32
+BF16 = mybir.dt.bfloat16
+I32 = mybir.dt.int32
+U32 = mybir.dt.uint32
+U8 = mybir.dt.uint8
+FP8X4 = mybir.dt.float8_e4m3fn_x4
+ALU = mybir.AluOpType
+ACT = mybir.ActivationFunctionType
+AXIS = mybir.AxisListType
+
+P = 128
+PACK = 4
+K_PASS = P * PACK
+BATCH = 6
+ROWS = 1024
+COLS = 1024
+WIDTH = 512
+X_PASSES = COLS // K_PASS
+HALVES = ROWS // K_PASS
+STEPS = BATCH * HALVES
+J_BLOCKS = WIDTH // P
+I_TILES = WIDTH // P
+EPS = 1e-5
+PREFETCH = 3
+
+FLOPS = 2 * BATCH * ROWS * COLS * WIDTH + 2 * BATCH * ROWS * WIDTH * WIDTH
+
+
+def tile_selfprojection_pa_kernel(
+    tc,
+    x,
+    xj_words,
+    xj_scales,
+    xi_words,
+    xi_scales,
+    gamma_o_sum,
+    gamma_o,
+    beta_o_sum,
+    beta_o,
+    out,
+    o_sum,
+):
+    nc = tc.nc
+    with ExitStack() as stack:
+        consts = stack.enter_context(tc.tile_pool(name="consts", bufs=1))
+        x_pool = stack.enter_context(tc.tile_pool(name="x_pool", bufs=PREFETCH + 1))
+        work = stack.enter_context(tc.tile_pool(name="work", bufs=2))
+        small = stack.enter_context(tc.tile_pool(name="small", bufs=2))
+        ring = stack.enter_context(tc.psum_pool(name="ring", bufs=6))
+        fixed = stack.enter_context(tc.psum_pool(name="fixed", bufs=1))
+
+        def load_x(step):
+            b, half = divmod(step, HALVES)
+            x_rows = x_pool.tile([P, PACK, COLS], BF16)
+            nc.sync.dma_start(
+                out=x_rows[:],
+                in_=x[b, K_PASS * half : K_PASS * (half + 1), :].rearrange(
+                    "(p t) n -> p t n", t=PACK
+                ),
+            )
+            return x_rows
+
+        def load_weight(words_in, scales_in, label):
+            words = consts.tile([P, HALVES, WIDTH], U32, name=label + "_words", align_bytes=64)
+            planes = consts.tile([P, HALVES, WIDTH], U8, name=label + "_planes", align_bytes=64)
+            nc.vector.memset(planes[:].bitcast(I32), 0)
+            for quadrant in range(4):
+                nc.sync.dma_start(
+                    out=planes[32 * quadrant : 32 * quadrant + 4].bitcast(I32),
+                    in_=scales_in[:, 4 * quadrant : 4 * quadrant + 4, :]
+                    .rearrange("g r n -> r g n")
+                    .bitcast(I32),
+                )
+            nc.sync.dma_start(
+                out=words[:].bitcast(I32),
+                in_=words_in.rearrange("g p n t -> p g (n t)").bitcast(I32),
+            )
+            return words, planes
+
+        x_rows_of = {0: load_x(0)}
+        wj_words, wj_planes = load_weight(xj_words, xj_scales, "wj")
+        x_rows_of[1] = load_x(1)
+        wi_words, wi_planes = load_weight(xi_words, xi_scales, "wi")
+        x_rows_of[2] = load_x(2)
+
+        identity = consts.tile([P, P], F32)
+        make_identity(nc, identity[:])
+        ones = consts.tile([P, P], F32)
+        nc.vector.memset(ones[:], 1.0)
+        selector = consts.tile([P, 2 * P], F32)
+        nc.vector.memset(selector[:], 0.0)
+        nc.vector.memset(selector[:, P : P + 1], 1.0)
+        one = consts.tile([P, 1], F32)
+        nc.vector.memset(one[:], 1.0)
+        warm = consts.tile([P, 1], F32)
+        nc.scalar.activation(out=warm[:], in_=one[:], func=ACT.Sqrt)
+
+        gamma = consts.tile([P, I_TILES, WIDTH], BF16)
+        nc.sync.dma_start(out=gamma[:], in_=gamma_o.rearrange("(i p) j -> p i j", p=P))
+        beta = consts.tile([P, I_TILES, WIDTH], BF16)
+        nc.sync.dma_start(out=beta[:], in_=beta_o.rearrange("(i p) j -> p i j", p=P))
+        gamma_sum = consts.tile([P, WIDTH], BF16)
+        nc.sync.dma_start(out=gamma_sum[0:BATCH], in_=gamma_o_sum.partition_broadcast(BATCH))
+        beta_sum = consts.tile([P, WIDTH], BF16)
+        nc.sync.dma_start(out=beta_sum[0:BATCH], in_=beta_o_sum.partition_broadcast(BATCH))
+
+        c_bank = fixed.tile([P, WIDTH], F32)
+
+        def transpose_and_quantise_x(step):
+            x_rows = x_rows_of[step]
+            x_grouped = work.tile([P, X_PASSES, K_PASS, PACK], BF16, align_bytes=64)
+            for c in range(X_PASSES):
+                for pair in range(2):
+                    xt_bank = ring.tile([P, 2, 2 * P], F32, tag="ring")
+                    for i in range(2):
+                        words = x_rows[:, 2 * pair + i, :].bitcast(F32)
+                        for u in range(2):
+                            nc.tensor.transpose(
+                                out=xt_bank[:, u, P * i : P * (i + 1)],
+                                in_=words[:, 256 * c + u : 256 * (c + 1) : 2],
+                                identity=identity[:],
+                            )
+                    nc.scalar.copy(
+                        out=x_grouped[:, c, 2 * P * pair : 2 * P * (pair + 1), :].bitcast(F32),
+                        in_=xt_bank[:].rearrange("q u m -> q m u"),
+                    )
+            x_words = work.tile([P, X_PASSES, K_PASS], U32, align_bytes=64)
+            x_planes = work.tile([P, X_PASSES, K_PASS], U8, align_bytes=64)
+            nc.vector.quantize_mx(
+                out=x_words[:].rearrange("q c m -> q (c m)").bitcast(FP8X4),
+                scales=x_planes[:].rearrange("q c m -> q (c m)"),
+                in_=x_grouped[:].rearrange("q c m t -> q (c m t)"),
+            )
+            return x_words, x_planes
+
+        def first_matmul(step, x_words, x_planes, y_words, y_planes, column_sums):
+            half = step % HALVES
+            y_grouped = work.tile([P, WIDTH, PACK], BF16, align_bytes=64)
+            for jb in range(J_BLOCKS):
+                j_cols = slice(P * jb, P * (jb + 1))
+                y_bank = ring.tile([P, PACK, P], F32, tag="ring")
+                for t in range(PACK):
+                    m_cols = slice(P * t, P * (t + 1))
+                    for c in range(X_PASSES):
+                        nc.tensor.matmul_mx(
+                            out=y_bank[:, t, :],
+                            lhsT=x_words[:, c, m_cols].bitcast(FP8X4),
+                            lhsT_scale=x_planes[:, c, m_cols],
+                            rhs=wj_words[:, c, j_cols].bitcast(FP8X4),
+                            rhs_scale=wj_planes[:, c, j_cols],
+                            start=(c == 0),
+                            stop=(c == X_PASSES - 1),
+                        )
+                four_rows = y_bank[:].rearrange("p t j -> p j t")
+                nc.scalar.copy(out=y_grouped[:, j_cols, :], in_=four_rows)
+                nc.vector.tensor_reduce(
+                    out=column_sums[:, half, j_cols], in_=four_rows, axis=AXIS.X, op=ALU.add
+                )
+            nc.vector.quantize_mx(
+                out=y_words[:, half, :].bitcast(FP8X4),
+                scales=y_planes[:, half, :],
+                in_=y_grouped[:].rearrange("p j t -> p (j t)"),
+            )
+
+        def add_column_sums(b, column_sums):
+            both_halves = work.tile([P, WIDTH], F32)
+            nc.vector.tensor_tensor(
+                out=both_halves[:], in0=column_sums[:, 0, :], in1=column_sums[:, 1, :], op=ALU.add
+            )
+            nc.tensor.matmul(
+                out=c_bank[:],
+                lhsT=selector[:, P - b : 2 * P - b],
+                rhs=both_halves[:],
+                start=(b == 0),
+                stop=(b == BATCH - 1),
+            )
+
+        def second_matmul(i_tiles, y_words, y_planes, z_rows, z_sums):
+            for i in i_tiles:
+                i_cols = slice(P * i, P * (i + 1))
+                z_bank = ring.tile([P, WIDTH], F32, tag="ring")
+                for half in range(HALVES):
+                    nc.tensor.matmul_mx(
+                        out=z_bank[:],
+                        lhsT=wi_words[:, half, i_cols].bitcast(FP8X4),
+                        lhsT_scale=wi_planes[:, half, i_cols],
+                        rhs=y_words[:, half, :].bitcast(FP8X4),
+                        rhs_scale=y_planes[:, half, :],
+                        start=(half == 0),
+                        stop=(half == HALVES - 1),
+                    )
+                nc.scalar.activation(
+                    out=z_rows[:, i, :], in_=z_bank[:], func=ACT.Copy, accum_out=z_sums[:, i : i + 1]
+                )
+                squares = work.tile([P, WIDTH], BF16, bufs=4)
+                nc.scalar.activation(
+                    out=squares[:],
+                    in_=z_rows[:, i, :],
+                    func=ACT.Square,
+                    accum_out=z_sums[:, I_TILES + i : I_TILES + i + 1],
+                )
+
+        def mean_and_std(total, total_of_squares, count, rows):
+            neg_mean = small.tile([P, 1], F32)
+            nc.vector.tensor_scalar(
+                out=neg_mean[0:rows], in0=total, scalar1=-1.0 / count, scalar2=None, op0=ALU.mult
+            )
+            deviations = small.tile([P, 1], F32)
+            nc.vector.scalar_tensor_tensor(
+                out=deviations[0:rows],
+                in0=total,
+                scalar=neg_mean[0:rows],
+                in1=total_of_squares,
+                op0=ALU.mult,
+                op1=ALU.add,
+            )
+            variance = small.tile([P, 1], F32)
+            nc.vector.tensor_scalar(
+                out=variance[0:rows],
+                in0=deviations[0:rows],
+                scalar1=1.0 / (count - 1),
+                scalar2=0.0,
+                op0=ALU.mult,
+                op1=ALU.max,
+            )
+            std = small.tile([P, 1], F32)
+            nc.scalar.activation(out=std[0:rows], in_=variance[0:rows], func=ACT.Sqrt)
+            std_eps = small.tile([P, 1], F32)
+            nc.vector.tensor_scalar(
+                out=std_eps[0:rows], in0=std[0:rows], scalar1=EPS, scalar2=None, op0=ALU.add
+            )
+            inv_std = small.tile([P, 1], F32)
+            nc.vector.reciprocal(out=inv_std[0:rows], in_=std_eps[0:rows])
+            return neg_mean, inv_std
+
+        def statistics(z_sums):
+            totals = fixed.tile([P, 2 * I_TILES], F32)
+            nc.tensor.matmul(out=totals[:], lhsT=ones[:], rhs=z_sums[:], start=True, stop=True)
+            sum_and_squares = small.tile([P, 2], F32)
+            nc.vector.tensor_reduce(
+                out=sum_and_squares[:],
+                in_=totals[:].rearrange("p (k i) -> p k i", k=2),
+                axis=AXIS.X,
+                op=ALU.add,
+            )
+            return mean_and_std(
+                sum_and_squares[:, 0:1], sum_and_squares[:, 1:2], WIDTH * WIDTH, P
+            )
+
+        def normalise(b, i_tiles, z_rows, neg_mean, inv_std):
+            result = work.tile([P, len(i_tiles), WIDTH], F32, bufs=3)
+            for i in i_tiles:
+                nc.vector.scalar_tensor_tensor(
+                    out=z_rows[:, i, :],
+                    in0=z_rows[:, i, :],
+                    scalar=neg_mean[:],
+                    in1=gamma[:, i, :],
+                    op0=ALU.add,
+                    op1=ALU.mult,
+                )
+            for k, i in enumerate(i_tiles):
+                nc.vector.scalar_tensor_tensor(
+                    out=result[:, k, :],
+                    in0=z_rows[:, i, :],
+                    scalar=inv_std[:],
+                    in1=beta[:, i, :],
+                    op0=ALU.mult,
+                    op1=ALU.add,
+                )
+                nc.sync.dma_start(out=out[b, P * i : P * (i + 1), :], in_=result[:, k, :])
+
+        def finish_o_sum():
+            c_rows = small.tile([P, WIDTH], F32)
+            c_sums = small.tile([P, 2], F32)
+            nc.scalar.activation(
+                out=c_rows[0:BATCH], in_=c_bank[0:BATCH], func=ACT.Copy, accum_out=c_sums[0:BATCH, 0:1]
+            )
+            c_squares = small.tile([P, WIDTH], BF16)
+            nc.scalar.activation(
+                out=c_squares[0:BATCH],
+                in_=c_rows[0:BATCH],
+                func=ACT.Square,
+                accum_out=c_sums[0:BATCH, 1:2],
+            )
+            neg_mean, inv_std = mean_and_std(
+                c_sums[0:BATCH, 0:1], c_sums[0:BATCH, 1:2], WIDTH, BATCH
+            )
+            c_normal = small.tile([P, WIDTH], F32)
+            nc.vector.tensor_scalar(
+                out=c_normal[0:BATCH],
+                in0=c_rows[0:BATCH],
+                scalar1=neg_mean[0:BATCH],
+                scalar2=inv_std[0:BATCH],
+                op0=ALU.add,
+                op1=ALU.mult,
+            )
+            c_scaled = small.tile([P, WIDTH], F32)
+            nc.vector.tensor_tensor(
+                out=c_scaled[0:BATCH], in0=c_normal[0:BATCH], in1=gamma_sum[0:BATCH], op=ALU.mult
+            )
+            c_result = small.tile([P, WIDTH], F32)
+            nc.vector.scalar_tensor_tensor(
+                out=c_result[0:BATCH],
+                in0=c_scaled[0:BATCH],
+                scalar=1.0,
+                in1=beta_sum[0:BATCH],
+                op0=ALU.add,
+                op1=ALU.add,
+            )
+            nc.sync.dma_start(out=o_sum[:, :], in_=c_result[0:BATCH])
+
+        FIRST = (0, 1)
+        SECOND = (2, 3)
+        quantised_x = {0: transpose_and_quantise_x(0)}
+        y_of = {}
+        z_of = {}
+        stats_of = {}
+        for step in range(STEPS):
+            b, half = divmod(step, HALVES)
+            if step + PREFETCH < STEPS:
+                x_rows_of[step + PREFETCH] = load_x(step + PREFETCH)
+            if step + 1 < STEPS:
+                quantised_x[step + 1] = transpose_and_quantise_x(step + 1)
+            if half == 0:
+                y_words = work.tile([P, HALVES, WIDTH], U32, align_bytes=64)
+                y_planes = work.tile([P, HALVES, WIDTH], U8, align_bytes=64)
+                column_sums = work.tile([P, HALVES, WIDTH], F32)
+                y_of[b] = (y_words, y_planes, column_sums)
+            y_words, y_planes, column_sums = y_of[b]
+            x_words, x_planes = quantised_x[step]
+            first_matmul(step, x_words, x_planes, y_words, y_planes, column_sums)
+            if half == 1:
+                add_column_sums(b, column_sums)
+            if b >= 1:
+                if half == 0:
+                    z_rows = work.tile([P, I_TILES, WIDTH], F32, bufs=3)
+                    z_sums = small.tile([P, 2 * I_TILES], F32)
+                    z_of[b - 1] = (z_rows, z_sums)
+                z_rows, z_sums = z_of[b - 1]
+                second_matmul((FIRST, SECOND)[half], y_of[b - 1][0], y_of[b - 1][1], z_rows, z_sums)
+                if half == 1:
+                    stats_of[b - 1] = statistics(z_sums)
+            if b >= 2:
+                neg_mean, inv_std = stats_of[b - 2]
+                normalise(b - 2, (FIRST, SECOND)[half], z_of[b - 2][0], neg_mean, inv_std)
+
+        last = BATCH - 1
+        z_rows = work.tile([P, I_TILES, WIDTH], F32, bufs=3)
+        z_sums = small.tile([P, 2 * I_TILES], F32)
+        second_matmul(FIRST + SECOND, y_of[last][0], y_of[last][1], z_rows, z_sums)
+        neg_mean, inv_std = stats_of[last - 1]
+        normalise(last - 1, FIRST, z_of[last - 1][0], neg_mean, inv_std)
+        normalise(last - 1, SECOND, z_of[last - 1][0], neg_mean, inv_std)
+        finish_o_sum()
+        neg_mean, inv_std = statistics(z_sums)
+        normalise(last, FIRST, z_rows, neg_mean, inv_std)
+        normalise(last, SECOND, z_rows, neg_mean, inv_std)

@@ -50,19 +50,19 @@ def tile_selfprojection_pa_kernel(
         consts = stack.enter_context(tc.tile_pool(name="consts", bufs=1))
         x_pool = stack.enter_context(tc.tile_pool(name="x_pool", bufs=PREFETCH + 1))
         work = stack.enter_context(tc.tile_pool(name="work", bufs=2))
-        small = stack.enter_context(tc.tile_pool(name="small", bufs=2))
+        small = stack.enter_context(tc.tile_pool(name="small", bufs=3))
         ring = stack.enter_context(tc.psum_pool(name="ring", bufs=6))
         fixed = stack.enter_context(tc.psum_pool(name="fixed", bufs=1))
+        stack.enter_context(tc.manual_schedule())
 
         def load_x(step):
             b, half = divmod(step, HALVES)
             x_rows = x_pool.tile([P, PACK, COLS], BF16)
-            nc.sync.dma_start(
-                out=x_rows[:],
-                in_=x[b, K_PASS * half : K_PASS * (half + 1), :].rearrange(
-                    "(p t) n -> p t n", t=PACK
-                ),
-            )
+            rows = x[b, K_PASS * half : K_PASS * (half + 1), :].rearrange("(p t) n -> p t n", t=PACK)
+            for pair in range(2):
+                nc.sync.dma_start(
+                    out=x_rows[:, 2 * pair : 2 * pair + 2, :], in_=rows[:, 2 * pair : 2 * pair + 2, :]
+                )
             return x_rows
 
         def load_weight(words_in, scales_in, label):
@@ -82,11 +82,10 @@ def tile_selfprojection_pa_kernel(
             )
             return words, planes
 
-        x_rows_of = {0: load_x(0)}
+        x_rows_of = {0: load_x(0), 1: load_x(1)}
         wj_words, wj_planes = load_weight(xj_words, xj_scales, "wj")
-        x_rows_of[1] = load_x(1)
-        wi_words, wi_planes = load_weight(xi_words, xi_scales, "wi")
         x_rows_of[2] = load_x(2)
+        wi_words, wi_planes = load_weight(xi_words, xi_scales, "wi")
 
         identity = consts.tile([P, P], F32)
         make_identity(nc, identity[:])
@@ -108,14 +107,23 @@ def tile_selfprojection_pa_kernel(
         nc.sync.dma_start(out=gamma_sum[0:BATCH], in_=gamma_o_sum.partition_broadcast(BATCH))
         beta_sum = consts.tile([P, WIDTH], BF16)
         nc.sync.dma_start(out=beta_sum[0:BATCH], in_=beta_o_sum.partition_broadcast(BATCH))
+        beta_sum_plus_one = consts.tile([P, WIDTH], F32)
+        nc.gpsimd.tensor_scalar(
+            out=beta_sum_plus_one[0:BATCH],
+            in0=beta_sum[0:BATCH],
+            scalar1=1.0,
+            scalar2=1.0,
+            op0=ALU.add,
+            op1=ALU.mult,
+        )
 
         c_bank = fixed.tile([P, WIDTH], F32)
 
-        def transpose_and_quantise_x(step):
+        def transpose_x(step):
             x_rows = x_rows_of[step]
             x_grouped = work.tile([P, X_PASSES, K_PASS, PACK], BF16, align_bytes=64)
-            for c in range(X_PASSES):
-                for pair in range(2):
+            for pair in range(2):
+                for c in range(X_PASSES):
                     xt_bank = ring.tile([P, 2, 2 * P], F32, tag="ring")
                     for i in range(2):
                         words = x_rows[:, 2 * pair + i, :].bitcast(F32)
@@ -125,10 +133,14 @@ def tile_selfprojection_pa_kernel(
                                 in_=words[:, 256 * c + u : 256 * (c + 1) : 2],
                                 identity=identity[:],
                             )
-                    nc.scalar.copy(
-                        out=x_grouped[:, c, 2 * P * pair : 2 * P * (pair + 1), :].bitcast(F32),
-                        in_=xt_bank[:].rearrange("q u m -> q m u"),
-                    )
+                    grouped_words = x_grouped[:, c, 2 * P * pair : 2 * P * (pair + 1), :].bitcast(F32)
+                    if pair == 1 and c == 1:
+                        nc.vector.tensor_copy(out=grouped_words, in_=xt_bank[:].rearrange("q u m -> q m u"))
+                    else:
+                        nc.scalar.copy(out=grouped_words, in_=xt_bank[:].rearrange("q u m -> q m u"))
+            return x_grouped
+
+        def quantise_x(x_grouped):
             x_words = work.tile([P, X_PASSES, K_PASS], U32, align_bytes=64)
             x_planes = work.tile([P, X_PASSES, K_PASS], U8, align_bytes=64)
             nc.vector.quantize_mx(
@@ -138,8 +150,7 @@ def tile_selfprojection_pa_kernel(
             )
             return x_words, x_planes
 
-        def first_matmul(step, x_words, x_planes, y_words, y_planes, column_sums):
-            half = step % HALVES
+        def first_matmul(half, x_words, x_planes, y_words, y_planes, column_sums):
             y_grouped = work.tile([P, WIDTH, PACK], BF16, align_bytes=64)
             for jb in range(J_BLOCKS):
                 j_cols = slice(P * jb, P * (jb + 1))
@@ -167,11 +178,14 @@ def tile_selfprojection_pa_kernel(
                 in_=y_grouped[:].rearrange("p j t -> p (j t)"),
             )
 
-        def add_column_sums(b, column_sums):
+        def add_halves(column_sums):
             both_halves = work.tile([P, WIDTH], F32)
             nc.vector.tensor_tensor(
                 out=both_halves[:], in0=column_sums[:, 0, :], in1=column_sums[:, 1, :], op=ALU.add
             )
+            return both_halves
+
+        def sum_over_partitions(b, both_halves):
             nc.tensor.matmul(
                 out=c_bank[:],
                 lhsT=selector[:, P - b : 2 * P - b],
@@ -197,6 +211,9 @@ def tile_selfprojection_pa_kernel(
                 nc.scalar.activation(
                     out=z_rows[:, i, :], in_=z_bank[:], func=ACT.Copy, accum_out=z_sums[:, i : i + 1]
                 )
+
+        def sum_squares(i_tiles, z_rows, z_sums):
+            for i in i_tiles:
                 squares = work.tile([P, WIDTH], BF16, bufs=4)
                 nc.scalar.activation(
                     out=squares[:],
@@ -205,11 +222,14 @@ def tile_selfprojection_pa_kernel(
                     accum_out=z_sums[:, I_TILES + i : I_TILES + i + 1],
                 )
 
-        def mean_and_std(total, total_of_squares, count, rows):
+        def negative_mean(total, count, rows):
             neg_mean = small.tile([P, 1], F32)
             nc.vector.tensor_scalar(
                 out=neg_mean[0:rows], in0=total, scalar1=-1.0 / count, scalar2=None, op0=ALU.mult
             )
+            return neg_mean
+
+        def unbiased_variance(total, neg_mean, total_of_squares, count, rows):
             deviations = small.tile([P, 1], F32)
             nc.vector.scalar_tensor_tensor(
                 out=deviations[0:rows],
@@ -228,6 +248,9 @@ def tile_selfprojection_pa_kernel(
                 op0=ALU.mult,
                 op1=ALU.max,
             )
+            return variance
+
+        def inverse_std(variance, rows):
             std = small.tile([P, 1], F32)
             nc.scalar.activation(out=std[0:rows], in_=variance[0:rows], func=ACT.Sqrt)
             std_eps = small.tile([P, 1], F32)
@@ -236,96 +259,88 @@ def tile_selfprojection_pa_kernel(
             )
             inv_std = small.tile([P, 1], F32)
             nc.vector.reciprocal(out=inv_std[0:rows], in_=std_eps[0:rows])
-            return neg_mean, inv_std
+            return inv_std
 
-        def statistics(z_sums):
+        def total_over_z(totals, z_sums, columns):
+            nc.tensor.matmul(
+                out=totals[:, columns], lhsT=ones[:], rhs=z_sums[:, columns], start=True, stop=True
+            )
+            total = small.tile([P, 1], F32, bufs=6)
+            nc.vector.tensor_reduce(out=total[:], in_=totals[:, columns], axis=AXIS.X, op=ALU.add)
+            return total
+
+        def z_mean(z_sums):
             totals = fixed.tile([P, 2 * I_TILES], F32)
-            nc.tensor.matmul(out=totals[:], lhsT=ones[:], rhs=z_sums[:], start=True, stop=True)
-            sum_and_squares = small.tile([P, 2], F32)
-            nc.vector.tensor_reduce(
-                out=sum_and_squares[:],
-                in_=totals[:].rearrange("p (k i) -> p k i", k=2),
-                axis=AXIS.X,
-                op=ALU.add,
-            )
-            return mean_and_std(
-                sum_and_squares[:, 0:1], sum_and_squares[:, 1:2], WIDTH * WIDTH, P
-            )
+            total = total_over_z(totals, z_sums, slice(0, I_TILES))
+            return totals, total, negative_mean(total[:], WIDTH * WIDTH, P)
 
-        def normalise(b, i_tiles, z_rows, neg_mean, inv_std):
-            result = work.tile([P, len(i_tiles), WIDTH], F32, bufs=3)
+        def z_variance(z_sums, totals, total, neg_mean):
+            total_of_squares = total_over_z(totals, z_sums, slice(I_TILES, 2 * I_TILES))
+            return unbiased_variance(total[:], neg_mean, total_of_squares[:], WIDTH * WIDTH, P)
+
+        def subtract_mean_and_gain(i_tiles, z_rows, neg_mean):
+            gained_of = {}
             for i in i_tiles:
+                gained = work.tile([P, WIDTH], F32, bufs=6)
                 nc.vector.scalar_tensor_tensor(
-                    out=z_rows[:, i, :],
+                    out=gained[:],
                     in0=z_rows[:, i, :],
                     scalar=neg_mean[:],
                     in1=gamma[:, i, :],
                     op0=ALU.add,
                     op1=ALU.mult,
                 )
-            for k, i in enumerate(i_tiles):
+                gained_of[i] = gained
+            return gained_of
+
+        def divide_by_std_and_bias(b, i_tiles, gained_of, inv_std):
+            for i in i_tiles:
+                result = work.tile([P, WIDTH], F32, bufs=6)
                 nc.vector.scalar_tensor_tensor(
-                    out=result[:, k, :],
-                    in0=z_rows[:, i, :],
+                    out=result[:],
+                    in0=gained_of[i][:],
                     scalar=inv_std[:],
                     in1=beta[:, i, :],
                     op0=ALU.mult,
                     op1=ALU.add,
                 )
-                nc.sync.dma_start(out=out[b, P * i : P * (i + 1), :], in_=result[:, k, :])
+                nc.sync.dma_start(out=out[b, P * i : P * (i + 1), :], in_=result[:])
 
-        def finish_o_sum():
-            c_rows = small.tile([P, WIDTH], F32)
-            c_sums = small.tile([P, 2], F32)
-            nc.scalar.activation(
-                out=c_rows[0:BATCH], in_=c_bank[0:BATCH], func=ACT.Copy, accum_out=c_sums[0:BATCH, 0:1]
-            )
-            c_squares = small.tile([P, WIDTH], BF16)
-            nc.scalar.activation(
-                out=c_squares[0:BATCH],
-                in_=c_rows[0:BATCH],
-                func=ACT.Square,
-                accum_out=c_sums[0:BATCH, 1:2],
-            )
-            neg_mean, inv_std = mean_and_std(
-                c_sums[0:BATCH, 0:1], c_sums[0:BATCH, 1:2], WIDTH, BATCH
-            )
-            c_normal = small.tile([P, WIDTH], F32)
-            nc.vector.tensor_scalar(
-                out=c_normal[0:BATCH],
-                in0=c_rows[0:BATCH],
-                scalar1=neg_mean[0:BATCH],
-                scalar2=inv_std[0:BATCH],
+        def normalise_on_gpsimd(b, i, z_rows, neg_mean, inv_std):
+            nc.gpsimd.tensor_scalar(
+                out=z_rows[:, i, :],
+                in0=z_rows[:, i, :],
+                scalar1=neg_mean[:],
+                scalar2=inv_std[:],
                 op0=ALU.add,
                 op1=ALU.mult,
             )
-            c_scaled = small.tile([P, WIDTH], F32)
-            nc.vector.tensor_tensor(
-                out=c_scaled[0:BATCH], in0=c_normal[0:BATCH], in1=gamma_sum[0:BATCH], op=ALU.mult
+            nc.gpsimd.tensor_tensor(
+                out=z_rows[:, i, :], in0=z_rows[:, i, :], in1=gamma[:, i, :], op=ALU.mult
             )
-            c_result = small.tile([P, WIDTH], F32)
-            nc.vector.scalar_tensor_tensor(
-                out=c_result[0:BATCH],
-                in0=c_scaled[0:BATCH],
-                scalar=1.0,
-                in1=beta_sum[0:BATCH],
-                op0=ALU.add,
-                op1=ALU.add,
-            )
-            nc.sync.dma_start(out=o_sum[:, :], in_=c_result[0:BATCH])
+            result = work.tile([P, WIDTH], F32, bufs=6)
+            nc.gpsimd.tensor_tensor(out=result[:], in0=z_rows[:, i, :], in1=beta[:, i, :], op=ALU.add)
+            nc.sync.dma_start(out=out[b, P * i : P * (i + 1), :], in_=result[:])
 
-        FIRST = (0, 1)
-        SECOND = (2, 3)
-        quantised_x = {0: transpose_and_quantise_x(0)}
+        quantised_x = {0: quantise_x(transpose_x(0))}
         y_of = {}
+        halves_of = {}
         z_of = {}
-        stats_of = {}
         for step in range(STEPS):
             b, half = divmod(step, HALVES)
             if step + PREFETCH < STEPS:
                 x_rows_of[step + PREFETCH] = load_x(step + PREFETCH)
             if step + 1 < STEPS:
-                quantised_x[step + 1] = transpose_and_quantise_x(step + 1)
+                x_grouped = transpose_x(step + 1)
+            if step >= HALVES + 1:
+                previous_b, previous_half = divmod(step - 1, HALVES)
+                sum_squares(
+                    (2 * previous_half, 2 * previous_half + 1),
+                    z_of[previous_b - 1][0],
+                    z_of[previous_b - 1][1],
+                )
+            if step + 1 < STEPS:
+                quantised_x[step + 1] = quantise_x(x_grouped)
             if half == 0:
                 y_words = work.tile([P, HALVES, WIDTH], U32, align_bytes=64)
                 y_planes = work.tile([P, HALVES, WIDTH], U8, align_bytes=64)
@@ -333,30 +348,84 @@ def tile_selfprojection_pa_kernel(
                 y_of[b] = (y_words, y_planes, column_sums)
             y_words, y_planes, column_sums = y_of[b]
             x_words, x_planes = quantised_x[step]
-            first_matmul(step, x_words, x_planes, y_words, y_planes, column_sums)
+            first_matmul(half, x_words, x_planes, y_words, y_planes, column_sums)
             if half == 1:
-                add_column_sums(b, column_sums)
+                halves_of[b] = add_halves(column_sums)
             if b >= 1:
                 if half == 0:
                     z_rows = work.tile([P, I_TILES, WIDTH], F32, bufs=3)
                     z_sums = small.tile([P, 2 * I_TILES], F32)
                     z_of[b - 1] = (z_rows, z_sums)
                 z_rows, z_sums = z_of[b - 1]
-                second_matmul((FIRST, SECOND)[half], y_of[b - 1][0], y_of[b - 1][1], z_rows, z_sums)
-                if half == 1:
-                    stats_of[b - 1] = statistics(z_sums)
+                second_matmul((2 * half, 2 * half + 1), y_of[b - 1][0], y_of[b - 1][1], z_rows, z_sums)
+            if half == 0 and b >= 1:
+                sum_over_partitions(b - 1, halves_of[b - 1])
+            if half == 0 and b >= 2:
+                z_rows, z_sums = z_of[b - 2]
+                totals, total, neg_mean = z_mean(z_sums)
+                variance = z_variance(z_sums, totals, total, neg_mean)
+                gained_of = subtract_mean_and_gain((0, 2), z_rows, neg_mean)
+                inv_std = inverse_std(variance, P)
             if b >= 2:
-                neg_mean, inv_std = stats_of[b - 2]
-                normalise(b - 2, (FIRST, SECOND)[half], z_of[b - 2][0], neg_mean, inv_std)
+                normalise_on_gpsimd(b - 2, 2 * half + 1, z_of[b - 2][0], neg_mean, inv_std)
+                divide_by_std_and_bias(b - 2, (2 * half,), gained_of, inv_std)
 
         last = BATCH - 1
-        z_rows = work.tile([P, I_TILES, WIDTH], F32, bufs=3)
-        z_sums = small.tile([P, 2 * I_TILES], F32)
-        second_matmul(FIRST + SECOND, y_of[last][0], y_of[last][1], z_rows, z_sums)
-        neg_mean, inv_std = stats_of[last - 1]
-        normalise(last - 1, FIRST, z_of[last - 1][0], neg_mean, inv_std)
-        normalise(last - 1, SECOND, z_of[last - 1][0], neg_mean, inv_std)
-        finish_o_sum()
-        neg_mean, inv_std = statistics(z_sums)
-        normalise(last, FIRST, z_rows, neg_mean, inv_std)
-        normalise(last, SECOND, z_rows, neg_mean, inv_std)
+        z_rows, z_sums = z_of[last - 1]
+        sum_squares((2, 3), z_rows, z_sums)
+        last_z_rows = work.tile([P, I_TILES, WIDTH], F32, name="z_rows", bufs=3)
+        last_z_sums = small.tile([P, 2 * I_TILES], F32, name="z_sums")
+        second_matmul((0, 1), y_of[last][0], y_of[last][1], last_z_rows, last_z_sums)
+        totals, total, neg_mean = z_mean(z_sums)
+        variance = z_variance(z_sums, totals, total, neg_mean)
+        gained_of = subtract_mean_and_gain((0, 2), z_rows, neg_mean)
+        inv_std = inverse_std(variance, P)
+        second_matmul((2, 3), y_of[last][0], y_of[last][1], last_z_rows, last_z_sums)
+        normalise_on_gpsimd(last - 1, 1, z_rows, neg_mean, inv_std)
+        normalise_on_gpsimd(last - 1, 3, z_rows, neg_mean, inv_std)
+        divide_by_std_and_bias(last - 1, (0, 2), gained_of, inv_std)
+
+        totals, total, neg_mean = z_mean(last_z_sums)
+        sum_squares((0, 1, 2, 3), last_z_rows, last_z_sums)
+        sum_over_partitions(last, halves_of[last])
+        gained_of = subtract_mean_and_gain((0, 1, 2, 3), last_z_rows, neg_mean)
+        variance = z_variance(last_z_sums, totals, total, neg_mean)
+
+        c_rows = small.tile([P, WIDTH], F32)
+        c_sums = small.tile([P, 2], F32)
+        nc.scalar.activation(
+            out=c_rows[0:BATCH], in_=c_bank[0:BATCH], func=ACT.Copy, accum_out=c_sums[0:BATCH, 0:1]
+        )
+        c_squares = small.tile([P, WIDTH], BF16)
+        nc.scalar.activation(
+            out=c_squares[0:BATCH],
+            in_=c_rows[0:BATCH],
+            func=ACT.Square,
+            accum_out=c_sums[0:BATCH, 1:2],
+        )
+        c_neg_mean = negative_mean(c_sums[0:BATCH, 0:1], WIDTH, BATCH)
+        c_variance = unbiased_variance(
+            c_sums[0:BATCH, 0:1], c_neg_mean, c_sums[0:BATCH, 1:2], WIDTH, BATCH
+        )
+        inv_std = inverse_std(variance, P)
+        c_inv_std = inverse_std(c_variance, BATCH)
+
+        c_normal = small.tile([P, WIDTH], F32)
+        nc.gpsimd.tensor_scalar(
+            out=c_normal[0:BATCH],
+            in0=c_rows[0:BATCH],
+            scalar1=c_neg_mean[0:BATCH],
+            scalar2=c_inv_std[0:BATCH],
+            op0=ALU.add,
+            op1=ALU.mult,
+        )
+        c_scaled = small.tile([P, WIDTH], F32)
+        nc.gpsimd.tensor_tensor(
+            out=c_scaled[0:BATCH], in0=c_normal[0:BATCH], in1=gamma_sum[0:BATCH], op=ALU.mult
+        )
+        c_result = small.tile([P, WIDTH], F32)
+        nc.gpsimd.tensor_tensor(
+            out=c_result[0:BATCH], in0=c_scaled[0:BATCH], in1=beta_sum_plus_one[0:BATCH], op=ALU.add
+        )
+        divide_by_std_and_bias(last, (0, 1, 2, 3), gained_of, inv_std)
+        nc.sync.dma_start(out=o_sum[:, :], in_=c_result[0:BATCH])

@@ -53,7 +53,6 @@ def tile_selfprojection_pa_kernel(
         small = stack.enter_context(tc.tile_pool(name="small", bufs=3))
         ring = stack.enter_context(tc.psum_pool(name="ring", bufs=6))
         fixed = stack.enter_context(tc.psum_pool(name="fixed", bufs=1))
-        stack.enter_context(tc.manual_schedule())
 
         def load_x(step):
             b, half = divmod(step, HALVES)
@@ -107,15 +106,6 @@ def tile_selfprojection_pa_kernel(
         nc.sync.dma_start(out=gamma_sum[0:BATCH], in_=gamma_o_sum.partition_broadcast(BATCH))
         beta_sum = consts.tile([P, WIDTH], BF16)
         nc.sync.dma_start(out=beta_sum[0:BATCH], in_=beta_o_sum.partition_broadcast(BATCH))
-        beta_sum_plus_one = consts.tile([P, WIDTH], F32)
-        nc.gpsimd.tensor_scalar(
-            out=beta_sum_plus_one[0:BATCH],
-            in0=beta_sum[0:BATCH],
-            scalar1=1.0,
-            scalar2=1.0,
-            op0=ALU.add,
-            op1=ALU.mult,
-        )
 
         c_bank = fixed.tile([P, WIDTH], F32)
 
@@ -134,10 +124,7 @@ def tile_selfprojection_pa_kernel(
                                 identity=identity[:],
                             )
                     grouped_words = x_grouped[:, c, 2 * P * pair : 2 * P * (pair + 1), :].bitcast(F32)
-                    if pair == 1 and c == 1:
-                        nc.vector.tensor_copy(out=grouped_words, in_=xt_bank[:].rearrange("q u m -> q m u"))
-                    else:
-                        nc.scalar.copy(out=grouped_words, in_=xt_bank[:].rearrange("q u m -> q m u"))
+                    nc.scalar.copy(out=grouped_words, in_=xt_bank[:].rearrange("q u m -> q m u"))
             return x_grouped
 
         def quantise_x(x_grouped):
@@ -281,7 +268,7 @@ def tile_selfprojection_pa_kernel(
         def subtract_mean_and_gain(i_tiles, z_rows, neg_mean):
             gained_of = {}
             for i in i_tiles:
-                gained = work.tile([P, WIDTH], F32, bufs=6)
+                gained = work.tile([P, WIDTH], F32, bufs=8)
                 nc.vector.scalar_tensor_tensor(
                     out=gained[:],
                     in0=z_rows[:, i, :],
@@ -306,41 +293,16 @@ def tile_selfprojection_pa_kernel(
                 )
                 nc.sync.dma_start(out=out[b, P * i : P * (i + 1), :], in_=result[:])
 
-        def normalise_on_gpsimd(b, i, z_rows, neg_mean, inv_std):
-            nc.gpsimd.tensor_scalar(
-                out=z_rows[:, i, :],
-                in0=z_rows[:, i, :],
-                scalar1=neg_mean[:],
-                scalar2=inv_std[:],
-                op0=ALU.add,
-                op1=ALU.mult,
-            )
-            nc.gpsimd.tensor_tensor(
-                out=z_rows[:, i, :], in0=z_rows[:, i, :], in1=gamma[:, i, :], op=ALU.mult
-            )
-            result = work.tile([P, WIDTH], F32, bufs=6)
-            nc.gpsimd.tensor_tensor(out=result[:], in0=z_rows[:, i, :], in1=beta[:, i, :], op=ALU.add)
-            nc.sync.dma_start(out=out[b, P * i : P * (i + 1), :], in_=result[:])
-
         quantised_x = {0: quantise_x(transpose_x(0))}
         y_of = {}
-        halves_of = {}
         z_of = {}
+        stats_of = {}
         for step in range(STEPS):
             b, half = divmod(step, HALVES)
             if step + PREFETCH < STEPS:
                 x_rows_of[step + PREFETCH] = load_x(step + PREFETCH)
             if step + 1 < STEPS:
-                x_grouped = transpose_x(step + 1)
-            if step >= HALVES + 1:
-                previous_b, previous_half = divmod(step - 1, HALVES)
-                sum_squares(
-                    (2 * previous_half, 2 * previous_half + 1),
-                    z_of[previous_b - 1][0],
-                    z_of[previous_b - 1][1],
-                )
-            if step + 1 < STEPS:
-                quantised_x[step + 1] = quantise_x(x_grouped)
+                quantised_x[step + 1] = quantise_x(transpose_x(step + 1))
             if half == 0:
                 y_words = work.tile([P, HALVES, WIDTH], U32, align_bytes=64)
                 y_planes = work.tile([P, HALVES, WIDTH], U8, align_bytes=64)
@@ -350,46 +312,40 @@ def tile_selfprojection_pa_kernel(
             x_words, x_planes = quantised_x[step]
             first_matmul(half, x_words, x_planes, y_words, y_planes, column_sums)
             if half == 1:
-                halves_of[b] = add_halves(column_sums)
+                sum_over_partitions(b, add_halves(column_sums))
             if b >= 1:
                 if half == 0:
                     z_rows = work.tile([P, I_TILES, WIDTH], F32, bufs=3)
                     z_sums = small.tile([P, 2 * I_TILES], F32)
                     z_of[b - 1] = (z_rows, z_sums)
                 z_rows, z_sums = z_of[b - 1]
-                second_matmul((2 * half, 2 * half + 1), y_of[b - 1][0], y_of[b - 1][1], z_rows, z_sums)
-            if half == 0 and b >= 1:
-                sum_over_partitions(b - 1, halves_of[b - 1])
-            if half == 0 and b >= 2:
-                z_rows, z_sums = z_of[b - 2]
-                totals, total, neg_mean = z_mean(z_sums)
-                variance = z_variance(z_sums, totals, total, neg_mean)
-                gained_of = subtract_mean_and_gain((0, 2), z_rows, neg_mean)
-                inv_std = inverse_std(variance, P)
+                i_tiles = (2 * half, 2 * half + 1)
+                second_matmul(i_tiles, y_of[b - 1][0], y_of[b - 1][1], z_rows, z_sums)
+                sum_squares(i_tiles, z_rows, z_sums)
+                if half == 1:
+                    totals, total, neg_mean = z_mean(z_sums)
+                    variance = z_variance(z_sums, totals, total, neg_mean)
+                    stats_of[b - 1] = (neg_mean, inverse_std(variance, P))
             if b >= 2:
-                normalise_on_gpsimd(b - 2, 2 * half + 1, z_of[b - 2][0], neg_mean, inv_std)
-                divide_by_std_and_bias(b - 2, (2 * half,), gained_of, inv_std)
+                neg_mean, inv_std = stats_of[b - 2]
+                i_tiles = (2 * half, 2 * half + 1)
+                gained_of = subtract_mean_and_gain(i_tiles, z_of[b - 2][0], neg_mean)
+                divide_by_std_and_bias(b - 2, i_tiles, gained_of, inv_std)
 
         last = BATCH - 1
-        z_rows, z_sums = z_of[last - 1]
-        sum_squares((2, 3), z_rows, z_sums)
+        all_tiles = (0, 1, 2, 3)
         last_z_rows = work.tile([P, I_TILES, WIDTH], F32, name="z_rows", bufs=3)
         last_z_sums = small.tile([P, 2 * I_TILES], F32, name="z_sums")
-        second_matmul((0, 1), y_of[last][0], y_of[last][1], last_z_rows, last_z_sums)
-        totals, total, neg_mean = z_mean(z_sums)
-        variance = z_variance(z_sums, totals, total, neg_mean)
-        gained_of = subtract_mean_and_gain((0, 2), z_rows, neg_mean)
-        inv_std = inverse_std(variance, P)
-        second_matmul((2, 3), y_of[last][0], y_of[last][1], last_z_rows, last_z_sums)
-        normalise_on_gpsimd(last - 1, 1, z_rows, neg_mean, inv_std)
-        normalise_on_gpsimd(last - 1, 3, z_rows, neg_mean, inv_std)
-        divide_by_std_and_bias(last - 1, (0, 2), gained_of, inv_std)
+        second_matmul(all_tiles, y_of[last][0], y_of[last][1], last_z_rows, last_z_sums)
+        totals, total, last_neg_mean = z_mean(last_z_sums)
+        sum_squares(all_tiles, last_z_rows, last_z_sums)
+        last_variance = z_variance(last_z_sums, totals, total, last_neg_mean)
+        last_inv_std = inverse_std(last_variance, P)
 
-        totals, total, neg_mean = z_mean(last_z_sums)
-        sum_squares((0, 1, 2, 3), last_z_rows, last_z_sums)
-        sum_over_partitions(last, halves_of[last])
-        gained_of = subtract_mean_and_gain((0, 1, 2, 3), last_z_rows, neg_mean)
-        variance = z_variance(last_z_sums, totals, total, neg_mean)
+        neg_mean, inv_std = stats_of[last - 1]
+        gained_of = subtract_mean_and_gain(all_tiles, z_of[last - 1][0], neg_mean)
+        divide_by_std_and_bias(last - 1, all_tiles, gained_of, inv_std)
+        gained_of = subtract_mean_and_gain(all_tiles, last_z_rows, last_neg_mean)
 
         c_rows = small.tile([P, WIDTH], F32)
         c_sums = small.tile([P, 2], F32)
@@ -407,11 +363,9 @@ def tile_selfprojection_pa_kernel(
         c_variance = unbiased_variance(
             c_sums[0:BATCH, 0:1], c_neg_mean, c_sums[0:BATCH, 1:2], WIDTH, BATCH
         )
-        inv_std = inverse_std(variance, P)
         c_inv_std = inverse_std(c_variance, BATCH)
-
         c_normal = small.tile([P, WIDTH], F32)
-        nc.gpsimd.tensor_scalar(
+        nc.vector.tensor_scalar(
             out=c_normal[0:BATCH],
             in0=c_rows[0:BATCH],
             scalar1=c_neg_mean[0:BATCH],
@@ -420,12 +374,18 @@ def tile_selfprojection_pa_kernel(
             op1=ALU.mult,
         )
         c_scaled = small.tile([P, WIDTH], F32)
-        nc.gpsimd.tensor_tensor(
+        nc.vector.tensor_tensor(
             out=c_scaled[0:BATCH], in0=c_normal[0:BATCH], in1=gamma_sum[0:BATCH], op=ALU.mult
         )
         c_result = small.tile([P, WIDTH], F32)
-        nc.gpsimd.tensor_tensor(
-            out=c_result[0:BATCH], in0=c_scaled[0:BATCH], in1=beta_sum_plus_one[0:BATCH], op=ALU.add
+        nc.vector.scalar_tensor_tensor(
+            out=c_result[0:BATCH],
+            in0=c_scaled[0:BATCH],
+            scalar=1.0,
+            in1=beta_sum[0:BATCH],
+            op0=ALU.add,
+            op1=ALU.add,
         )
-        divide_by_std_and_bias(last, (0, 1, 2, 3), gained_of, inv_std)
         nc.sync.dma_start(out=o_sum[:, :], in_=c_result[0:BATCH])
+
+        divide_by_std_and_bias(last, all_tiles, gained_of, last_inv_std)

@@ -26,7 +26,7 @@ STEPS = BATCH * HALVES
 J_BLOCKS = WIDTH // P
 I_TILES = WIDTH // P
 EPS = 1e-5
-PREFETCH = 3
+PREFETCH = 4
 
 FLOPS = 2 * BATCH * ROWS * COLS * WIDTH + 2 * BATCH * ROWS * WIDTH * WIDTH
 
@@ -51,17 +51,18 @@ def tile_selfprojection_pa_kernel(
         x_pool = stack.enter_context(tc.tile_pool(name="x_pool", bufs=PREFETCH + 1))
         work = stack.enter_context(tc.tile_pool(name="work", bufs=2))
         small = stack.enter_context(tc.tile_pool(name="small", bufs=3))
-        ring = stack.enter_context(tc.psum_pool(name="ring", bufs=6))
-        fixed = stack.enter_context(tc.psum_pool(name="fixed", bufs=1))
+        ring = stack.enter_context(tc.psum_pool(name="ring", bufs=4))
+        z_pool = stack.enter_context(tc.psum_pool(name="z_pool", bufs=I_TILES))
 
         def load_x(step):
             b, half = divmod(step, HALVES)
             x_rows = x_pool.tile([P, PACK, COLS], BF16)
             rows = x[b, K_PASS * half : K_PASS * (half + 1), :].rearrange("(p t) n -> p t n", t=PACK)
-            for pair in range(2):
-                nc.sync.dma_start(
-                    out=x_rows[:, 2 * pair : 2 * pair + 2, :], in_=rows[:, 2 * pair : 2 * pair + 2, :]
-                )
+            width = K_PASS if step == 0 else COLS
+            for c in range(COLS // width):
+                for v in range(2):
+                    piece = (slice(0, P), slice(2 * v, 2 * v + 2), slice(width * c, width * (c + 1)))
+                    nc.sync.dma_start(out=x_rows[piece], in_=rows[piece])
             return x_rows
 
         def load_weight(words_in, scales_in, label):
@@ -81,22 +82,26 @@ def tile_selfprojection_pa_kernel(
             )
             return words, planes
 
-        x_rows_of = {0: load_x(0), 1: load_x(1)}
+        x_rows_of = {0: load_x(0)}
         wj_words, wj_planes = load_weight(xj_words, xj_scales, "wj")
+        x_rows_of[1] = load_x(1)
         x_rows_of[2] = load_x(2)
         wi_words, wi_planes = load_weight(xi_words, xi_scales, "wi")
+        x_rows_of[3] = load_x(3)
 
         identity = consts.tile([P, P], F32)
         make_identity(nc, identity[:])
-        ones = consts.tile([P, P], F32)
-        nc.vector.memset(ones[:], 1.0)
-        selector = consts.tile([P, 2 * P], F32)
-        nc.vector.memset(selector[:], 0.0)
-        nc.vector.memset(selector[:, P : P + 1], 1.0)
+        averager = consts.tile([P, P], F32)
+        nc.gpsimd.memset(averager[:], 1.0 / P)
+        minus_one = consts.tile([P, 1], F32)
+        nc.gpsimd.memset(minus_one[:], -1.0)
         one = consts.tile([P, 1], F32)
         nc.vector.memset(one[:], 1.0)
         warm = consts.tile([P, 1], F32)
         nc.scalar.activation(out=warm[:], in_=one[:], func=ACT.Sqrt)
+        c_parts = consts.tile([P, BATCH, J_BLOCKS, HALVES], F32)
+        c_columns = consts.tile([P, J_BLOCKS, P], F32)
+        nc.gpsimd.memset(c_columns[:], 0.0)
 
         gamma = consts.tile([P, I_TILES, WIDTH], BF16)
         nc.sync.dma_start(out=gamma[:], in_=gamma_o.rearrange("(i p) j -> p i j", p=P))
@@ -106,140 +111,139 @@ def tile_selfprojection_pa_kernel(
         nc.sync.dma_start(out=gamma_sum[0:BATCH], in_=gamma_o_sum.partition_broadcast(BATCH))
         beta_sum = consts.tile([P, WIDTH], BF16)
         nc.sync.dma_start(out=beta_sum[0:BATCH], in_=beta_o_sum.partition_broadcast(BATCH))
-
-        c_bank = fixed.tile([P, WIDTH], F32)
+        beta_sum_one = consts.tile([P, WIDTH], F32)
+        nc.gpsimd.tensor_scalar(
+            out=beta_sum_one[0:BATCH], in0=beta_sum[0:BATCH], scalar1=1.0, scalar2=None, op0=ALU.add
+        )
 
         def transpose_x(step):
             x_rows = x_rows_of[step]
             x_grouped = work.tile([P, X_PASSES, K_PASS, PACK], BF16, align_bytes=64)
-            for pair in range(2):
-                for c in range(X_PASSES):
+            for c in range(X_PASSES):
+                for v in range(2):
                     xt_bank = ring.tile([P, 2, 2 * P], F32, tag="ring")
-                    for i in range(2):
-                        words = x_rows[:, 2 * pair + i, :].bitcast(F32)
+                    for e in range(2):
+                        words = x_rows[:, 2 * v + e, :].bitcast(F32)
                         for u in range(2):
                             nc.tensor.transpose(
-                                out=xt_bank[:, u, P * i : P * (i + 1)],
+                                out=xt_bank[:, u, P * e : P * (e + 1)],
                                 in_=words[:, 256 * c + u : 256 * (c + 1) : 2],
                                 identity=identity[:],
                             )
-                    grouped_words = x_grouped[:, c, 2 * P * pair : 2 * P * (pair + 1), :].bitcast(F32)
-                    nc.scalar.copy(out=grouped_words, in_=xt_bank[:].rearrange("q u m -> q m u"))
+                    grouped_words = x_grouped[:, c, 2 * P * v : 2 * P * (v + 1), :].bitcast(F32)
+                    copy = nc.vector.tensor_copy if step == 0 and v == 1 else nc.scalar.copy
+                    copy(
+                        out=grouped_words.rearrange("q (p e) u -> q p e u", e=2),
+                        in_=xt_bank[:].rearrange("q u (e p) -> q p e u", e=2),
+                    )
             return x_grouped
 
-        def quantise_x(x_grouped):
+        def quantise_x(x_grouped, calls=1):
             x_words = work.tile([P, X_PASSES, K_PASS], U32, align_bytes=64)
             x_planes = work.tile([P, X_PASSES, K_PASS], U8, align_bytes=64)
-            nc.vector.quantize_mx(
-                out=x_words[:].rearrange("q c m -> q (c m)").bitcast(FP8X4),
-                scales=x_planes[:].rearrange("q c m -> q (c m)"),
-                in_=x_grouped[:].rearrange("q c m t -> q (c m t)"),
-            )
+            passes = X_PASSES // calls
+            for call in range(calls):
+                some = slice(passes * call, passes * (call + 1))
+                nc.vector.quantize_mx(
+                    out=x_words[:, some, :].rearrange("q c m -> q (c m)").bitcast(FP8X4),
+                    scales=x_planes[:, some, :].rearrange("q c m -> q (c m)"),
+                    in_=x_grouped[:, some, :, :].rearrange("q c m t -> q (c m t)"),
+                )
             return x_words, x_planes
 
-        def first_matmul(half, x_words, x_planes, y_words, y_planes, column_sums):
-            y_grouped = work.tile([P, WIDTH, PACK], BF16, align_bytes=64)
-            for jb in range(J_BLOCKS):
+        def first_matmul(step, j_blocks, x_words, x_planes, y_columns):
+            b, half = divmod(step, HALVES)
+            for jb in j_blocks:
                 j_cols = slice(P * jb, P * (jb + 1))
-                y_bank = ring.tile([P, PACK, P], F32, tag="ring")
-                for t in range(PACK):
-                    m_cols = slice(P * t, P * (t + 1))
-                    for c in range(X_PASSES):
-                        nc.tensor.matmul_mx(
-                            out=y_bank[:, t, :],
-                            lhsT=x_words[:, c, m_cols].bitcast(FP8X4),
-                            lhsT_scale=x_planes[:, c, m_cols],
-                            rhs=wj_words[:, c, j_cols].bitcast(FP8X4),
-                            rhs_scale=wj_planes[:, c, j_cols],
-                            start=(c == 0),
-                            stop=(c == X_PASSES - 1),
-                        )
-                four_rows = y_bank[:].rearrange("p t j -> p j t")
-                nc.scalar.copy(out=y_grouped[:, j_cols, :], in_=four_rows)
-                nc.vector.tensor_reduce(
-                    out=column_sums[:, half, j_cols], in_=four_rows, axis=AXIS.X, op=ALU.add
-                )
-            nc.vector.quantize_mx(
-                out=y_words[:, half, :].bitcast(FP8X4),
-                scales=y_planes[:, half, :],
-                in_=y_grouped[:].rearrange("p j t -> p (j t)"),
-            )
-
-        def add_halves(column_sums):
-            both_halves = work.tile([P, WIDTH], F32)
-            nc.vector.tensor_tensor(
-                out=both_halves[:], in0=column_sums[:, 0, :], in1=column_sums[:, 1, :], op=ALU.add
-            )
-            return both_halves
-
-        def sum_over_partitions(b, both_halves):
-            nc.tensor.matmul(
-                out=c_bank[:],
-                lhsT=selector[:, P - b : 2 * P - b],
-                rhs=both_halves[:],
-                start=(b == 0),
-                stop=(b == BATCH - 1),
-            )
-
-        def second_matmul(i_tiles, y_words, y_planes, z_rows, z_sums):
-            for i in i_tiles:
-                i_cols = slice(P * i, P * (i + 1))
-                z_bank = ring.tile([P, WIDTH], F32, tag="ring")
-                for half in range(HALVES):
+                y_bank = ring.tile([P, K_PASS], F32, tag="ring")
+                for c in range(X_PASSES):
                     nc.tensor.matmul_mx(
-                        out=z_bank[:],
-                        lhsT=wi_words[:, half, i_cols].bitcast(FP8X4),
-                        lhsT_scale=wi_planes[:, half, i_cols],
-                        rhs=y_words[:, half, :].bitcast(FP8X4),
-                        rhs_scale=y_planes[:, half, :],
-                        start=(half == 0),
-                        stop=(half == HALVES - 1),
+                        out=y_bank[:],
+                        lhsT=wj_words[:, c, j_cols].bitcast(FP8X4),
+                        lhsT_scale=wj_planes[:, c, j_cols],
+                        rhs=x_words[:, c, :].bitcast(FP8X4),
+                        rhs_scale=x_planes[:, c, :],
+                        start=(c == 0),
+                        stop=(c == X_PASSES - 1),
                     )
                 nc.scalar.activation(
-                    out=z_rows[:, i, :], in_=z_bank[:], func=ACT.Copy, accum_out=z_sums[:, i : i + 1]
+                    out=y_columns[:, jb, :],
+                    in_=y_bank[:],
+                    func=ACT.Copy,
+                    accum_out=c_parts[:, b, jb, half : half + 1],
                 )
 
-        def sum_squares(i_tiles, z_rows, z_sums):
-            for i in i_tiles:
-                squares = work.tile([P, WIDTH], BF16, bufs=4)
-                nc.scalar.activation(
-                    out=squares[:],
-                    in_=z_rows[:, i, :],
-                    func=ACT.Square,
-                    accum_out=z_sums[:, I_TILES + i : I_TILES + i + 1],
-                )
+        def transpose_y(half, y_columns, y_grouped):
+            for pair in range(J_BLOCKS // 2):
+                yt_bank = ring.tile([P, 2, 2 * P], F32, tag="ring")
+                for i in range(2):
+                    words = y_columns[:, 2 * pair + i, :].bitcast(F32)
+                    for v in range(2):
+                        nc.tensor.transpose(
+                            out=yt_bank[:, v, P * i : P * (i + 1)],
+                            in_=words[:, P * v : P * (v + 1)],
+                            identity=identity[:],
+                        )
+                grouped_words = y_grouped[:, half, 2 * P * pair : 2 * P * (pair + 1), :].bitcast(F32)
+                nc.scalar.copy(out=grouped_words, in_=yt_bank[:].rearrange("p v j -> p j v"))
 
-        def negative_mean(total, count, rows):
-            neg_mean = small.tile([P, 1], F32)
-            nc.vector.tensor_scalar(
-                out=neg_mean[0:rows], in0=total, scalar1=-1.0 / count, scalar2=None, op0=ALU.mult
+        def quantise_y(halves, y_grouped, y_words, y_planes):
+            nc.vector.quantize_mx(
+                out=y_words[:, halves, :].rearrange("p h j -> p (h j)").bitcast(FP8X4),
+                scales=y_planes[:, halves, :].rearrange("p h j -> p (h j)"),
+                in_=y_grouped[:, halves, :, :].rearrange("p h j t -> p (h j t)"),
             )
-            return neg_mean
 
-        def unbiased_variance(total, neg_mean, total_of_squares, count, rows):
-            deviations = small.tile([P, 1], F32)
+        def second_matmul(i, z_bank, y_words, y_planes):
+            i_cols = slice(P * i, P * (i + 1))
+            for half in range(HALVES):
+                nc.tensor.matmul_mx(
+                    out=z_bank[:],
+                    lhsT=wi_words[:, half, i_cols].bitcast(FP8X4),
+                    lhsT_scale=wi_planes[:, half, i_cols],
+                    rhs=y_words[:, half, :].bitcast(FP8X4),
+                    rhs_scale=y_planes[:, half, :],
+                    start=(half == 0),
+                    stop=(half == HALVES - 1),
+                )
+
+        def row_statistics(i, z_bank, stats):
+            nc.vector.bn_stats(out=stats[:, i, :], in_=z_bank[:])
+
+        def row_moments(stats):
+            moments = small.tile([P, 2], F32)
+            nc.vector.bn_aggr(out=moments[:], in_=stats[:].rearrange("p i s -> p (i s)"))
             nc.vector.scalar_tensor_tensor(
-                out=deviations[0:rows],
-                in0=total,
-                scalar=neg_mean[0:rows],
-                in1=total_of_squares,
+                out=moments[:, 1:2],
+                in0=moments[:, 0:1],
+                scalar=moments[:, 0:1],
+                in1=moments[:, 1:2],
                 op0=ALU.mult,
                 op1=ALU.add,
             )
-            variance = small.tile([P, 1], F32)
+            return moments
+
+        def total_moments(moments, totals):
+            nc.tensor.matmul(out=totals[:], lhsT=averager[:], rhs=moments[:], start=True, stop=True)
+
+        def unbiased_variance(neg_variance, count, rows):
+            unbiased = small.tile([P, 1], F32)
             nc.vector.tensor_scalar(
-                out=variance[0:rows],
-                in0=deviations[0:rows],
-                scalar1=1.0 / (count - 1),
+                out=unbiased[0:rows],
+                in0=neg_variance,
+                scalar1=-count / (count - 1),
                 scalar2=0.0,
                 op0=ALU.mult,
                 op1=ALU.max,
             )
-            return variance
+            return unbiased
 
-        def inverse_std(variance, rows):
+        def square_root(variance, rows):
             std = small.tile([P, 1], F32)
             nc.scalar.activation(out=std[0:rows], in_=variance[0:rows], func=ACT.Sqrt)
+            return std
+
+        def inverse(std, rows):
             std_eps = small.tile([P, 1], F32)
             nc.vector.tensor_scalar(
                 out=std_eps[0:rows], in0=std[0:rows], scalar1=EPS, scalar2=None, op0=ALU.add
@@ -248,144 +252,206 @@ def tile_selfprojection_pa_kernel(
             nc.vector.reciprocal(out=inv_std[0:rows], in_=std_eps[0:rows])
             return inv_std
 
-        def total_over_z(totals, z_sums, columns):
-            nc.tensor.matmul(
-                out=totals[:, columns], lhsT=ones[:], rhs=z_sums[:, columns], start=True, stop=True
+        def mean_and_variance(totals):
+            neg_mean = small.tile([P, 1], F32)
+            nc.vector.tensor_scalar(
+                out=neg_mean[:], in0=totals[:, 0:1], scalar1=-1.0, scalar2=None, op0=ALU.mult
             )
-            total = small.tile([P, 1], F32, bufs=6)
-            nc.vector.tensor_reduce(out=total[:], in_=totals[:, columns], axis=AXIS.X, op=ALU.add)
-            return total
+            neg_variance = small.tile([P, 1], F32)
+            nc.vector.scalar_tensor_tensor(
+                out=neg_variance[:],
+                in0=neg_mean[:],
+                scalar=neg_mean[:],
+                in1=totals[:, 1:2],
+                op0=ALU.mult,
+                op1=ALU.subtract,
+            )
+            return neg_mean, unbiased_variance(neg_variance[:], WIDTH * WIDTH, P)
 
-        def z_mean(z_sums):
-            totals = fixed.tile([P, 2 * I_TILES], F32)
-            total = total_over_z(totals, z_sums, slice(0, I_TILES))
-            return totals, total, negative_mean(total[:], WIDTH * WIDTH, P)
+        def subtract_mean_and_gain(i, z_bank, neg_mean):
+            gained = work.tile([P, WIDTH], F32, bufs=8)
+            nc.vector.scalar_tensor_tensor(
+                out=gained[:],
+                in0=z_bank[:],
+                scalar=neg_mean[:],
+                in1=gamma[:, i, :],
+                op0=ALU.add,
+                op1=ALU.mult,
+            )
+            return gained
 
-        def z_variance(z_sums, totals, total, neg_mean):
-            total_of_squares = total_over_z(totals, z_sums, slice(I_TILES, 2 * I_TILES))
-            return unbiased_variance(total[:], neg_mean, total_of_squares[:], WIDTH * WIDTH, P)
+        def divide_by_std_and_bias(b, i, gained, inv_std):
+            result = work.tile([P, WIDTH], F32, bufs=6)
+            nc.vector.scalar_tensor_tensor(
+                out=result[:],
+                in0=gained[:],
+                scalar=inv_std[:],
+                in1=beta[:, i, :],
+                op0=ALU.mult,
+                op1=ALU.add,
+            )
+            nc.sync.dma_start(out=out[b, P * i : P * (i + 1), :], in_=result[:])
 
-        def subtract_mean_and_gain(i_tiles, z_rows, neg_mean):
-            gained_of = {}
-            for i in i_tiles:
-                gained = work.tile([P, WIDTH], F32, bufs=8)
-                nc.vector.scalar_tensor_tensor(
-                    out=gained[:],
-                    in0=z_rows[:, i, :],
-                    scalar=neg_mean[:],
-                    in1=gamma[:, i, :],
-                    op0=ALU.add,
-                    op1=ALU.mult,
-                )
-                gained_of[i] = gained
-            return gained_of
-
-        def divide_by_std_and_bias(b, i_tiles, gained_of, inv_std):
-            for i in i_tiles:
-                result = work.tile([P, WIDTH], F32, bufs=6)
-                nc.vector.scalar_tensor_tensor(
-                    out=result[:],
-                    in0=gained_of[i][:],
-                    scalar=inv_std[:],
-                    in1=beta[:, i, :],
-                    op0=ALU.mult,
-                    op1=ALU.add,
-                )
-                nc.sync.dma_start(out=out[b, P * i : P * (i + 1), :], in_=result[:])
-
-        quantised_x = {0: quantise_x(transpose_x(0))}
-        y_of = {}
-        z_of = {}
-        stats_of = {}
-        for step in range(STEPS):
-            b, half = divmod(step, HALVES)
-            if step + PREFETCH < STEPS:
-                x_rows_of[step + PREFETCH] = load_x(step + PREFETCH)
-            if step + 1 < STEPS:
-                quantised_x[step + 1] = quantise_x(transpose_x(step + 1))
-            if half == 0:
+        stack.enter_context(tc.manual_schedule())
+        last = BATCH - 1
+        all_halves = slice(0, HALVES)
+        quantised_x = {0: quantise_x(transpose_x(0), calls=X_PASSES)}
+        y_columns_of = {}
+        gained = []
+        for b in range(BATCH):
+            first, second = HALVES * b, HALVES * b + 1
+            for step in (first + PREFETCH, second + PREFETCH):
+                if step < STEPS:
+                    x_rows_of[step] = load_x(step)
+            if b >= 2:
+                inv_std = inverse(std, P)
+            if b >= 1:
+                y_grouped = work.tile([P, HALVES, WIDTH, PACK], BF16, align_bytes=64)
                 y_words = work.tile([P, HALVES, WIDTH], U32, align_bytes=64)
                 y_planes = work.tile([P, HALVES, WIDTH], U8, align_bytes=64)
-                column_sums = work.tile([P, HALVES, WIDTH], F32)
-                y_of[b] = (y_words, y_planes, column_sums)
-            y_words, y_planes, column_sums = y_of[b]
-            x_words, x_planes = quantised_x[step]
-            first_matmul(half, x_words, x_planes, y_words, y_planes, column_sums)
-            if half == 1:
-                sum_over_partitions(b, add_halves(column_sums))
-            if b >= 1:
-                if half == 0:
-                    z_rows = work.tile([P, I_TILES, WIDTH], F32, bufs=3)
-                    z_sums = small.tile([P, 2 * I_TILES], F32)
-                    z_of[b - 1] = (z_rows, z_sums)
-                z_rows, z_sums = z_of[b - 1]
-                i_tiles = (2 * half, 2 * half + 1)
-                second_matmul(i_tiles, y_of[b - 1][0], y_of[b - 1][1], z_rows, z_sums)
-                sum_squares(i_tiles, z_rows, z_sums)
-                if half == 1:
-                    totals, total, neg_mean = z_mean(z_sums)
-                    variance = z_variance(z_sums, totals, total, neg_mean)
-                    stats_of[b - 1] = (neg_mean, inverse_std(variance, P))
+                transpose_y(0, y_columns_of[first - 2], y_grouped)
+                transpose_y(1, y_columns_of[first - 1], y_grouped)
             if b >= 2:
-                neg_mean, inv_std = stats_of[b - 2]
-                i_tiles = (2 * half, 2 * half + 1)
-                gained_of = subtract_mean_and_gain(i_tiles, z_of[b - 2][0], neg_mean)
-                divide_by_std_and_bias(b - 2, i_tiles, gained_of, inv_std)
+                divide_by_std_and_bias(b - 2, 0, gained[0], inv_std)
+                divide_by_std_and_bias(b - 2, 1, gained[1], inv_std)
+            if b >= 1:
+                quantise_y(all_halves, y_grouped, y_words, y_planes)
+            y_columns_of[first] = work.tile([P, J_BLOCKS, K_PASS], BF16, name="y_columns", bufs=4)
+            first_matmul(first, range(J_BLOCKS), *quantised_x[first], y_columns_of[first])
+            if b >= 2:
+                divide_by_std_and_bias(b - 2, 2, gained[2], inv_std)
+                divide_by_std_and_bias(b - 2, 3, gained[3], inv_std)
+            quantised_x[second] = quantise_x(transpose_x(second))
+            if b >= 1:
+                z_banks = []
+                stats = small.tile([P, I_TILES, 6], F32)
+                for i in range(I_TILES):
+                    z_bank = z_pool.tile([P, WIDTH], F32)
+                    second_matmul(i, z_bank, y_words, y_planes)
+                    row_statistics(i, z_bank, stats)
+                    z_banks.append(z_bank)
+                moments = row_moments(stats)
+            if b < last:
+                quantised_x[second + 1] = quantise_x(transpose_x(second + 1))
+            y_columns_of[second] = work.tile([P, J_BLOCKS, K_PASS], BF16, name="y_columns", bufs=4)
+            first_matmul(second, (0, 1), *quantised_x[second], y_columns_of[second])
+            if b == last:
+                first_matmul(second, (2, 3), *quantised_x[second], y_columns_of[second])
+                last_y_grouped = work.tile([P, HALVES, WIDTH, PACK], BF16, name="y_grouped", align_bytes=64)
+                transpose_y(0, y_columns_of[first], last_y_grouped)
+            if b >= 1:
+                totals = ring.tile([P, 2], F32, tag="ring")
+                total_moments(moments, totals)
+                neg_mean, variance = mean_and_variance(totals)
+                now = range(1 if b == last else I_TILES)
+                gained = [subtract_mean_and_gain(i, z_banks[i], neg_mean) for i in now]
+            if b < last:
+                first_matmul(second, (2, 3), *quantised_x[second], y_columns_of[second])
+            if b >= 1:
+                std = square_root(variance, P)
 
-        last = BATCH - 1
-        all_tiles = (0, 1, 2, 3)
-        last_z_rows = work.tile([P, I_TILES, WIDTH], F32, name="z_rows", bufs=3)
-        last_z_sums = small.tile([P, 2 * I_TILES], F32, name="z_sums")
-        second_matmul(all_tiles, y_of[last][0], y_of[last][1], last_z_rows, last_z_sums)
-        totals, total, last_neg_mean = z_mean(last_z_sums)
-        sum_squares(all_tiles, last_z_rows, last_z_sums)
-        last_variance = z_variance(last_z_sums, totals, total, last_neg_mean)
-        last_inv_std = inverse_std(last_variance, P)
+        y_words = work.tile([P, HALVES, WIDTH], U32, align_bytes=64)
+        y_planes = work.tile([P, HALVES, WIDTH], U8, align_bytes=64)
+        quantise_y(slice(0, 1), last_y_grouped, y_words, y_planes)
+        transpose_y(1, y_columns_of[STEPS - 1], last_y_grouped)
+        nc.gpsimd.tensor_tensor(
+            out=c_columns[:, :, 0:BATCH],
+            in0=c_parts[:, :, :, 0].rearrange("p b k -> p k b"),
+            in1=c_parts[:, :, :, 1].rearrange("p b k -> p k b"),
+            op=ALU.add,
+        )
+        gained.append(subtract_mean_and_gain(1, z_banks[1], neg_mean))
+        inv_std = inverse(std, P)
+        quantise_y(slice(1, 2), last_y_grouped, y_words, y_planes)
+        gained.extend([subtract_mean_and_gain(i, z_banks[i], neg_mean) for i in (2, 3)])
+        c_bank = ring.tile([P, J_BLOCKS, P], F32, tag="ring")
+        for jb in range(J_BLOCKS):
+            nc.tensor.transpose(out=c_bank[:, jb, :], in_=c_columns[:, jb, :], identity=identity[:])
+        for i in range(I_TILES):
+            scaled = work.tile([P, WIDTH], F32, bufs=4)
+            nc.scalar.activation(out=scaled[:], in_=gained[i][:], func=ACT.Copy, scale=inv_std[:])
+            result = work.tile([P, WIDTH], F32, bufs=6)
+            nc.gpsimd.tensor_tensor(out=result[:], in0=scaled[:], in1=beta[:, i, :], op=ALU.add)
+            nc.sync.dma_start(out=out[last - 1, P * i : P * (i + 1), :], in_=result[:])
+            if i == 0:
+                c_rows = c_bank[0:BATCH].rearrange("b k j -> b (k j)")
+                c_sums = small.tile([P, 2], F32)
+                c_copy = small.tile([P, WIDTH], F32)
+                nc.scalar.activation(
+                    out=c_copy[0:BATCH], in_=c_rows, func=ACT.Copy, accum_out=c_sums[0:BATCH, 0:1]
+                )
+                c_squares = small.tile([P, WIDTH], F32)
+                nc.scalar.activation(
+                    out=c_squares[0:BATCH],
+                    in_=c_copy[0:BATCH],
+                    func=ACT.Square,
+                    accum_out=c_sums[0:BATCH, 1:2],
+                )
+        z_banks = []
+        stats = small.tile([P, I_TILES, 6], F32)
+        for i in range(I_TILES):
+            z_bank = z_pool.tile([P, WIDTH], F32)
+            second_matmul(i, z_bank, y_words, y_planes)
+            row_statistics(i, z_bank, stats)
+            z_banks.append(z_bank)
+        moments = row_moments(stats)
+        totals = ring.tile([P, 2], F32, tag="ring")
+        total_moments(moments, totals)
+        neg_mean, variance = mean_and_variance(totals)
+        std = square_root(variance, P)
+        gained = [subtract_mean_and_gain(i, z_banks[i], neg_mean) for i in (0, 1)]
+        inv_std = inverse(std, P)
+        divide_by_std_and_bias(last, 0, gained[0], inv_std)
+        divide_by_std_and_bias(last, 1, gained[1], inv_std)
+        for i in (2, 3):
+            gained.append(subtract_mean_and_gain(i, z_banks[i], neg_mean))
+            divide_by_std_and_bias(last, i, gained[i], inv_std)
 
-        neg_mean, inv_std = stats_of[last - 1]
-        gained_of = subtract_mean_and_gain(all_tiles, z_of[last - 1][0], neg_mean)
-        divide_by_std_and_bias(last - 1, all_tiles, gained_of, inv_std)
-        gained_of = subtract_mean_and_gain(all_tiles, last_z_rows, last_neg_mean)
-
-        c_rows = small.tile([P, WIDTH], F32)
-        c_sums = small.tile([P, 2], F32)
-        nc.scalar.activation(
-            out=c_rows[0:BATCH], in_=c_bank[0:BATCH], func=ACT.Copy, accum_out=c_sums[0:BATCH, 0:1]
+        c_moments = small.tile([P, 2], F32)
+        nc.gpsimd.tensor_scalar(
+            out=c_moments[0:BATCH], in0=c_sums[0:BATCH], scalar1=1.0 / WIDTH, scalar2=0.0, op0=ALU.mult, op1=ALU.add
         )
-        c_squares = small.tile([P, WIDTH], BF16)
-        nc.scalar.activation(
-            out=c_squares[0:BATCH],
-            in_=c_rows[0:BATCH],
-            func=ACT.Square,
-            accum_out=c_sums[0:BATCH, 1:2],
+        c_mean_square = small.tile([P, 1], F32)
+        nc.gpsimd.tensor_tensor(
+            out=c_mean_square[0:BATCH], in0=c_moments[0:BATCH, 0:1], in1=c_moments[0:BATCH, 0:1], op=ALU.mult
         )
-        c_neg_mean = negative_mean(c_sums[0:BATCH, 0:1], WIDTH, BATCH)
-        c_variance = unbiased_variance(
-            c_sums[0:BATCH, 0:1], c_neg_mean, c_sums[0:BATCH, 1:2], WIDTH, BATCH
+        c_spread = small.tile([P, 1], F32)
+        nc.gpsimd.tensor_tensor(
+            out=c_spread[0:BATCH], in0=c_moments[0:BATCH, 1:2], in1=c_mean_square[0:BATCH], op=ALU.subtract
         )
-        c_inv_std = inverse_std(c_variance, BATCH)
+        c_variance = small.tile([P, 1], F32)
+        nc.gpsimd.tensor_scalar(
+            out=c_variance[0:BATCH],
+            in0=c_spread[0:BATCH],
+            scalar1=WIDTH / (WIDTH - 1),
+            scalar2=0.0,
+            op0=ALU.mult,
+            op1=ALU.max,
+        )
+        c_std = square_root(c_variance, BATCH)
+        c_std_eps = small.tile([P, 1], F32)
+        nc.gpsimd.tensor_scalar(
+            out=c_std_eps[0:BATCH], in0=c_std[0:BATCH], scalar1=EPS, scalar2=None, op0=ALU.add
+        )
+        c_inv_std = small.tile([P, 1], F32)
+        nc.gpsimd.tensor_tensor(
+            out=c_inv_std[0:BATCH], in0=c_std_eps[0:BATCH], in1=minus_one[0:BATCH], op=ALU.pow
+        )
         c_normal = small.tile([P, WIDTH], F32)
-        nc.vector.tensor_scalar(
+        nc.gpsimd.tensor_scalar(
             out=c_normal[0:BATCH],
-            in0=c_rows[0:BATCH],
-            scalar1=c_neg_mean[0:BATCH],
+            in0=c_copy[0:BATCH],
+            scalar1=c_moments[0:BATCH, 0:1],
             scalar2=c_inv_std[0:BATCH],
-            op0=ALU.add,
+            op0=ALU.subtract,
             op1=ALU.mult,
         )
         c_scaled = small.tile([P, WIDTH], F32)
-        nc.vector.tensor_tensor(
+        nc.gpsimd.tensor_tensor(
             out=c_scaled[0:BATCH], in0=c_normal[0:BATCH], in1=gamma_sum[0:BATCH], op=ALU.mult
         )
         c_result = small.tile([P, WIDTH], F32)
-        nc.vector.scalar_tensor_tensor(
-            out=c_result[0:BATCH],
-            in0=c_scaled[0:BATCH],
-            scalar=1.0,
-            in1=beta_sum[0:BATCH],
-            op0=ALU.add,
-            op1=ALU.add,
+        nc.gpsimd.tensor_tensor(
+            out=c_result[0:BATCH], in0=c_scaled[0:BATCH], in1=beta_sum_one[0:BATCH], op=ALU.add
         )
-        nc.sync.dma_start(out=o_sum[:, :], in_=c_result[0:BATCH])
-
-        divide_by_std_and_bias(last, all_tiles, gained_of, last_inv_std)
+        nc.gpsimd.dma_start(out=o_sum[:, :], in_=c_result[0:BATCH])

@@ -59,8 +59,8 @@ def tile_selfprojection_pa_kernel(
             x_rows = x_pool.tile([P, PACK, COLS], BF16)
             rows = x[b, K_PASS * half : K_PASS * (half + 1), :].rearrange("(p t) n -> p t n", t=PACK)
             width = K_PASS if step == 0 else COLS
-            for c in range(COLS // width):
-                for v in range(2):
+            for v in range(2):
+                for c in range(COLS // width):
                     piece = (slice(0, P), slice(2 * v, 2 * v + 2), slice(width * c, width * (c + 1)))
                     nc.sync.dma_start(out=x_rows[piece], in_=rows[piece])
             return x_rows
@@ -93,8 +93,6 @@ def tile_selfprojection_pa_kernel(
         make_identity(nc, identity[:])
         averager = consts.tile([P, P], F32)
         nc.gpsimd.memset(averager[:], 1.0 / P)
-        minus_one = consts.tile([P, 1], F32)
-        nc.gpsimd.memset(minus_one[:], -1.0)
         one = consts.tile([P, 1], F32)
         nc.vector.memset(one[:], 1.0)
         warm = consts.tile([P, 1], F32)
@@ -116,27 +114,24 @@ def tile_selfprojection_pa_kernel(
             out=beta_sum_one[0:BATCH], in0=beta_sum[0:BATCH], scalar1=1.0, scalar2=None, op0=ALU.add
         )
 
-        def transpose_x(step):
+        def transpose_x(step, v, x_grouped):
             x_rows = x_rows_of[step]
-            x_grouped = work.tile([P, X_PASSES, K_PASS, PACK], BF16, align_bytes=64)
             for c in range(X_PASSES):
-                for v in range(2):
-                    xt_bank = ring.tile([P, 2, 2 * P], F32, tag="ring")
-                    for e in range(2):
-                        words = x_rows[:, 2 * v + e, :].bitcast(F32)
-                        for u in range(2):
-                            nc.tensor.transpose(
-                                out=xt_bank[:, u, P * e : P * (e + 1)],
-                                in_=words[:, 256 * c + u : 256 * (c + 1) : 2],
-                                identity=identity[:],
-                            )
-                    grouped_words = x_grouped[:, c, 2 * P * v : 2 * P * (v + 1), :].bitcast(F32)
-                    copy = nc.vector.tensor_copy if step == 0 and v == 1 else nc.scalar.copy
-                    copy(
-                        out=grouped_words.rearrange("q (p e) u -> q p e u", e=2),
-                        in_=xt_bank[:].rearrange("q u (e p) -> q p e u", e=2),
-                    )
-            return x_grouped
+                xt_bank = ring.tile([P, 2, 2 * P], F32, tag="ring")
+                for e in range(2):
+                    words = x_rows[:, 2 * v + e, :].bitcast(F32)
+                    for u in range(2):
+                        nc.tensor.transpose(
+                            out=xt_bank[:, u, P * e : P * (e + 1)],
+                            in_=words[:, 256 * c + u : 256 * (c + 1) : 2],
+                            identity=identity[:],
+                        )
+                grouped_words = x_grouped[:, c, 2 * P * v : 2 * P * (v + 1), :].bitcast(F32)
+                copy = nc.vector.tensor_copy if step == 0 and c == 1 else nc.scalar.copy
+                copy(
+                    out=grouped_words.rearrange("q (p e) u -> q p e u", e=2),
+                    in_=xt_bank[:].rearrange("q u (e p) -> q p e u", e=2),
+                )
 
         def quantise_x(x_grouped, calls=1):
             x_words = work.tile([P, X_PASSES, K_PASS], U32, align_bytes=64)
@@ -173,25 +168,24 @@ def tile_selfprojection_pa_kernel(
                     accum_out=c_parts[:, b, jb, half : half + 1],
                 )
 
-        def transpose_y(half, y_columns, y_grouped):
-            for pair in range(J_BLOCKS // 2):
-                yt_bank = ring.tile([P, 2, 2 * P], F32, tag="ring")
-                for i in range(2):
-                    words = y_columns[:, 2 * pair + i, :].bitcast(F32)
-                    for v in range(2):
-                        nc.tensor.transpose(
-                            out=yt_bank[:, v, P * i : P * (i + 1)],
-                            in_=words[:, P * v : P * (v + 1)],
-                            identity=identity[:],
-                        )
-                grouped_words = y_grouped[:, half, 2 * P * pair : 2 * P * (pair + 1), :].bitcast(F32)
-                nc.scalar.copy(out=grouped_words, in_=yt_bank[:].rearrange("p v j -> p j v"))
+        def transpose_y(half, pair, y_columns, y_grouped):
+            yt_bank = ring.tile([P, 2, 2 * P], F32, tag="ring")
+            for i in range(2):
+                words = y_columns[:, 2 * pair + i, :].bitcast(F32)
+                for v in range(2):
+                    nc.tensor.transpose(
+                        out=yt_bank[:, v, P * i : P * (i + 1)],
+                        in_=words[:, P * v : P * (v + 1)],
+                        identity=identity[:],
+                    )
+            grouped_words = y_grouped[:, half, 2 * P * pair : 2 * P * (pair + 1), :].bitcast(F32)
+            nc.scalar.copy(out=grouped_words, in_=yt_bank[:].rearrange("p v j -> p j v"))
 
-        def quantise_y(halves, y_grouped, y_words, y_planes):
+        def quantise_y(half, y_grouped, y_words, y_planes):
             nc.vector.quantize_mx(
-                out=y_words[:, halves, :].rearrange("p h j -> p (h j)").bitcast(FP8X4),
-                scales=y_planes[:, halves, :].rearrange("p h j -> p (h j)"),
-                in_=y_grouped[:, halves, :, :].rearrange("p h j t -> p (h j t)"),
+                out=y_words[:, half, :].bitcast(FP8X4),
+                scales=y_planes[:, half, :],
+                in_=y_grouped[:, half, :, :].rearrange("p j t -> p (j t)"),
             )
 
         def second_matmul(i, z_bank, y_words, y_planes):
@@ -292,108 +286,154 @@ def tile_selfprojection_pa_kernel(
             )
             nc.sync.dma_start(out=out[b, P * i : P * (i + 1), :], in_=result[:])
 
-        stack.enter_context(tc.manual_schedule())
         last = BATCH - 1
-        all_halves = slice(0, HALVES)
-        quantised_x = {0: quantise_x(transpose_x(0), calls=X_PASSES)}
+
+        def new_y_operand():
+            return (
+                work.tile([P, HALVES, WIDTH, PACK], BF16, name="y_grouped", align_bytes=64),
+                work.tile([P, HALVES, WIDTH], U32, name="y_words", align_bytes=64),
+                work.tile([P, HALVES, WIDTH], U8, name="y_planes", align_bytes=64),
+            )
+
+        def second_matmuls(i_tiles, y_operand, z_banks):
+            for i in i_tiles:
+                z_bank = z_pool.tile([P, WIDTH], F32)
+                second_matmul(i, z_bank, y_operand[1], y_operand[2])
+                z_banks.append(z_bank)
+
+        def all_row_statistics(i_tiles, z_banks, stats):
+            for i in i_tiles:
+                row_statistics(i, z_banks[i], stats)
+
+        def new_x_grouped():
+            return work.tile([P, X_PASSES, K_PASS, PACK], BF16, name="x_grouped", align_bytes=64)
+
+        x_grouped = new_x_grouped()
+        for v in range(2):
+            transpose_x(0, v, x_grouped)
+        quantised_x = {0: quantise_x(x_grouped)}
         y_columns_of = {}
+        y_operand_of = {}
+        z_banks = []
         gained = []
         for b in range(BATCH):
             first, second = HALVES * b, HALVES * b + 1
             for step in (first + PREFETCH, second + PREFETCH):
                 if step < STEPS:
                     x_rows_of[step] = load_x(step)
-            if b >= 2:
-                inv_std = inverse(std, P)
-            if b >= 1:
-                y_grouped = work.tile([P, HALVES, WIDTH, PACK], BF16, align_bytes=64)
-                y_words = work.tile([P, HALVES, WIDTH], U32, align_bytes=64)
-                y_planes = work.tile([P, HALVES, WIDTH], U8, align_bytes=64)
-                transpose_y(0, y_columns_of[first - 2], y_grouped)
-                transpose_y(1, y_columns_of[first - 1], y_grouped)
-            if b >= 2:
-                divide_by_std_and_bias(b - 2, 0, gained[0], inv_std)
-                divide_by_std_and_bias(b - 2, 1, gained[1], inv_std)
-            if b >= 1:
-                quantise_y(all_halves, y_grouped, y_words, y_planes)
-            y_columns_of[first] = work.tile([P, J_BLOCKS, K_PASS], BF16, name="y_columns", bufs=4)
-            first_matmul(first, range(J_BLOCKS), *quantised_x[first], y_columns_of[first])
-            if b >= 2:
-                divide_by_std_and_bias(b - 2, 2, gained[2], inv_std)
-                divide_by_std_and_bias(b - 2, 3, gained[3], inv_std)
-            quantised_x[second] = quantise_x(transpose_x(second))
-            if b >= 1:
-                z_banks = []
-                stats = small.tile([P, I_TILES, 6], F32)
-                for i in range(I_TILES):
-                    z_bank = z_pool.tile([P, WIDTH], F32)
-                    second_matmul(i, z_bank, y_words, y_planes)
-                    row_statistics(i, z_bank, stats)
-                    z_banks.append(z_bank)
-                moments = row_moments(stats)
-            if b < last:
-                quantised_x[second + 1] = quantise_x(transpose_x(second + 1))
-            y_columns_of[second] = work.tile([P, J_BLOCKS, K_PASS], BF16, name="y_columns", bufs=4)
-            first_matmul(second, (0, 1), *quantised_x[second], y_columns_of[second])
-            if b == last:
-                first_matmul(second, (2, 3), *quantised_x[second], y_columns_of[second])
-                last_y_grouped = work.tile([P, HALVES, WIDTH, PACK], BF16, name="y_grouped", align_bytes=64)
-                transpose_y(0, y_columns_of[first], last_y_grouped)
-            if b >= 1:
-                totals = ring.tile([P, 2], F32, tag="ring")
-                total_moments(moments, totals)
-                neg_mean, variance = mean_and_variance(totals)
-                now = range(1 if b == last else I_TILES)
-                gained = [subtract_mean_and_gain(i, z_banks[i], neg_mean) for i in now]
-            if b < last:
-                first_matmul(second, (2, 3), *quantised_x[second], y_columns_of[second])
-            if b >= 1:
-                std = square_root(variance, P)
+            y_operand_of[b] = new_y_operand()
+            for half in range(HALVES):
+                step = HALVES * b + half
+                y_columns_of[step] = work.tile([P, J_BLOCKS, K_PASS], BF16, name="y_columns", bufs=4)
+                if half == 1 and b >= 1:
+                    z_banks = []
+                    stats = small.tile([P, I_TILES, 6], F32, name="stats")
+                if step + 1 < STEPS:
+                    x_grouped = new_x_grouped()
+                for part in range(2):
+                    if step + 1 < STEPS:
+                        transpose_x(step + 1, part, x_grouped)
+                    if half == 0 and b >= 1:
+                        transpose_y(1, part, y_columns_of[first - 1], y_operand_of[b - 1][0])
+                    if half == 1:
+                        transpose_y(0, part, y_columns_of[first], y_operand_of[b][0])
+                    first_matmul(step, (2 * part, 2 * part + 1), *quantised_x[step], y_columns_of[step])
+                    if half == 1 and b >= 1:
+                        second_matmuls((2 * part, 2 * part + 1), y_operand_of[b - 1], z_banks)
+                    if half == 0 and part == 0 and b >= 2:
+                        moments = row_moments(stats)
+                        totals = ring.tile([P, 2], F32, tag="ring")
+                        total_moments(moments, totals)
+                        neg_mean, variance = mean_and_variance(totals)
+                        gained = [subtract_mean_and_gain(i, z_banks[i], neg_mean) for i in (0, 1)]
+                    if half == 0 and part == 1:
+                        if b >= 1:
+                            quantise_y(1, *y_operand_of[b - 1])
+                        if b >= 2:
+                            gained.extend(
+                                [subtract_mean_and_gain(i, z_banks[i], neg_mean) for i in (2, 3)]
+                            )
+                            std = square_root(variance, P)
+                        quantised_x[step + 1] = quantise_x(x_grouped)
+                    if half == 1 and part == 0:
+                        if b >= 2:
+                            inv_std = inverse(std, P)
+                            divide_by_std_and_bias(b - 2, 0, gained[0], inv_std)
+                            divide_by_std_and_bias(b - 2, 1, gained[1], inv_std)
+                        if b >= 1:
+                            all_row_statistics((0, 1), z_banks, stats)
+                    if half == 1 and part == 1:
+                        if b >= 2:
+                            divide_by_std_and_bias(b - 2, 2, gained[2], inv_std)
+                            divide_by_std_and_bias(b - 2, 3, gained[3], inv_std)
+                        if step + 1 < STEPS:
+                            quantised_x[step + 1] = quantise_x(x_grouped)
+                        quantise_y(0, *y_operand_of[b])
+                        if b >= 1:
+                            all_row_statistics((2, 3), z_banks, stats)
 
-        y_words = work.tile([P, HALVES, WIDTH], U32, align_bytes=64)
-        y_planes = work.tile([P, HALVES, WIDTH], U8, align_bytes=64)
-        quantise_y(slice(0, 1), last_y_grouped, y_words, y_planes)
-        transpose_y(1, y_columns_of[STEPS - 1], last_y_grouped)
+        moments = row_moments(stats)
+        for part in range(2):
+            transpose_y(1, part, y_columns_of[STEPS - 1], y_operand_of[last][0])
         nc.gpsimd.tensor_tensor(
             out=c_columns[:, :, 0:BATCH],
             in0=c_parts[:, :, :, 0].rearrange("p b k -> p k b"),
             in1=c_parts[:, :, :, 1].rearrange("p b k -> p k b"),
             op=ALU.add,
         )
-        gained.append(subtract_mean_and_gain(1, z_banks[1], neg_mean))
+        totals = ring.tile([P, 2], F32, tag="ring")
+        total_moments(moments, totals)
+        neg_mean, variance = mean_and_variance(totals)
+        gained = [subtract_mean_and_gain(i, z_banks[i], neg_mean) for i in (0, 1)]
+        std = square_root(variance, P)
+        quantise_y(1, *y_operand_of[last])
         inv_std = inverse(std, P)
-        quantise_y(slice(1, 2), last_y_grouped, y_words, y_planes)
         gained.extend([subtract_mean_and_gain(i, z_banks[i], neg_mean) for i in (2, 3)])
         c_bank = ring.tile([P, J_BLOCKS, P], F32, tag="ring")
         for jb in range(J_BLOCKS):
             nc.tensor.transpose(out=c_bank[:, jb, :], in_=c_columns[:, jb, :], identity=identity[:])
+        c_rows = c_bank[0:BATCH].rearrange("b k j -> b (k j)")
         for i in range(I_TILES):
             scaled = work.tile([P, WIDTH], F32, bufs=4)
             nc.scalar.activation(out=scaled[:], in_=gained[i][:], func=ACT.Copy, scale=inv_std[:])
             result = work.tile([P, WIDTH], F32, bufs=6)
             nc.gpsimd.tensor_tensor(out=result[:], in0=scaled[:], in1=beta[:, i, :], op=ALU.add)
             nc.sync.dma_start(out=out[last - 1, P * i : P * (i + 1), :], in_=result[:])
-            if i == 0:
-                c_rows = c_bank[0:BATCH].rearrange("b k j -> b (k j)")
-                c_sums = small.tile([P, 2], F32)
-                c_copy = small.tile([P, WIDTH], F32)
-                nc.scalar.activation(
-                    out=c_copy[0:BATCH], in_=c_rows, func=ACT.Copy, accum_out=c_sums[0:BATCH, 0:1]
-                )
-                c_squares = small.tile([P, WIDTH], F32)
-                nc.scalar.activation(
-                    out=c_squares[0:BATCH],
-                    in_=c_copy[0:BATCH],
-                    func=ACT.Square,
-                    accum_out=c_sums[0:BATCH, 1:2],
-                )
         z_banks = []
         stats = small.tile([P, I_TILES, 6], F32)
-        for i in range(I_TILES):
-            z_bank = z_pool.tile([P, WIDTH], F32)
-            second_matmul(i, z_bank, y_words, y_planes)
-            row_statistics(i, z_bank, stats)
-            z_banks.append(z_bank)
+        second_matmuls(range(I_TILES), y_operand_of[last], z_banks)
+        c_stats = small.tile([P, 6], F32)
+        nc.vector.bn_stats(out=c_stats[0:BATCH], in_=c_rows)
+        c_moments = small.tile([P, 2], F32)
+        nc.vector.bn_aggr(out=c_moments[0:BATCH], in_=c_stats[0:BATCH])
+        c_variance = small.tile([P, 1], F32)
+        nc.vector.tensor_scalar(
+            out=c_variance[0:BATCH],
+            in0=c_moments[0:BATCH, 1:2],
+            scalar1=WIDTH / (WIDTH - 1),
+            scalar2=None,
+            op0=ALU.mult,
+        )
+        c_std = square_root(c_variance, BATCH)
+        all_row_statistics((0, 1, 2, 3), z_banks, stats)
+        c_inv_std = inverse(c_std, BATCH)
+        c_shift = small.tile([P, 1], F32)
+        nc.vector.scalar_tensor_tensor(
+            out=c_shift[0:BATCH],
+            in0=c_moments[0:BATCH, 0:1],
+            scalar=-1.0,
+            in1=c_inv_std[0:BATCH],
+            op0=ALU.mult,
+            op1=ALU.mult,
+        )
+        c_normal = small.tile([P, WIDTH], F32)
+        nc.scalar.activation(
+            out=c_normal[0:BATCH],
+            in_=c_rows,
+            func=ACT.Identity,
+            scale=c_inv_std[0:BATCH],
+            bias=c_shift[0:BATCH],
+        )
         moments = row_moments(stats)
         totals = ring.tile([P, 2], F32, tag="ring")
         total_moments(moments, totals)
@@ -406,46 +446,6 @@ def tile_selfprojection_pa_kernel(
         for i in (2, 3):
             gained.append(subtract_mean_and_gain(i, z_banks[i], neg_mean))
             divide_by_std_and_bias(last, i, gained[i], inv_std)
-
-        c_moments = small.tile([P, 2], F32)
-        nc.gpsimd.tensor_scalar(
-            out=c_moments[0:BATCH], in0=c_sums[0:BATCH], scalar1=1.0 / WIDTH, scalar2=0.0, op0=ALU.mult, op1=ALU.add
-        )
-        c_mean_square = small.tile([P, 1], F32)
-        nc.gpsimd.tensor_tensor(
-            out=c_mean_square[0:BATCH], in0=c_moments[0:BATCH, 0:1], in1=c_moments[0:BATCH, 0:1], op=ALU.mult
-        )
-        c_spread = small.tile([P, 1], F32)
-        nc.gpsimd.tensor_tensor(
-            out=c_spread[0:BATCH], in0=c_moments[0:BATCH, 1:2], in1=c_mean_square[0:BATCH], op=ALU.subtract
-        )
-        c_variance = small.tile([P, 1], F32)
-        nc.gpsimd.tensor_scalar(
-            out=c_variance[0:BATCH],
-            in0=c_spread[0:BATCH],
-            scalar1=WIDTH / (WIDTH - 1),
-            scalar2=0.0,
-            op0=ALU.mult,
-            op1=ALU.max,
-        )
-        c_std = square_root(c_variance, BATCH)
-        c_std_eps = small.tile([P, 1], F32)
-        nc.gpsimd.tensor_scalar(
-            out=c_std_eps[0:BATCH], in0=c_std[0:BATCH], scalar1=EPS, scalar2=None, op0=ALU.add
-        )
-        c_inv_std = small.tile([P, 1], F32)
-        nc.gpsimd.tensor_tensor(
-            out=c_inv_std[0:BATCH], in0=c_std_eps[0:BATCH], in1=minus_one[0:BATCH], op=ALU.pow
-        )
-        c_normal = small.tile([P, WIDTH], F32)
-        nc.gpsimd.tensor_scalar(
-            out=c_normal[0:BATCH],
-            in0=c_copy[0:BATCH],
-            scalar1=c_moments[0:BATCH, 0:1],
-            scalar2=c_inv_std[0:BATCH],
-            op0=ALU.subtract,
-            op1=ALU.mult,
-        )
         c_scaled = small.tile([P, WIDTH], F32)
         nc.gpsimd.tensor_tensor(
             out=c_scaled[0:BATCH], in0=c_normal[0:BATCH], in1=gamma_sum[0:BATCH], op=ALU.mult

@@ -286,6 +286,7 @@ def tile_selfprojection_pa_kernel(
             )
             nc.sync.dma_start(out=out[b, P * i : P * (i + 1), :], in_=result[:])
 
+        stack.enter_context(tc.manual_schedule(engines={mybir.EngineType.PE}))
         last = BATCH - 1
 
         def new_y_operand():

@@ -54,19 +54,19 @@ def tile_selfprojection_pa_kernel(
         ring = stack.enter_context(tc.psum_pool(name="ring", bufs=4))
         z_pool = stack.enter_context(tc.psum_pool(name="z_pool", bufs=I_TILES))
 
-        def load_x(step):
+        def load_x(step, v_parts=(0, 1)):
             b, half = divmod(step, HALVES)
-            x_rows = x_pool.tile([P, PACK, COLS], BF16)
+            if step not in x_rows_of:
+                x_rows_of[step] = x_pool.tile([P, PACK, COLS], BF16, name="x_rows")
+            x_rows = x_rows_of[step]
             rows = x[b, K_PASS * half : K_PASS * (half + 1), :].rearrange("(p t) n -> p t n", t=PACK)
             width = K_PASS if step == 0 else COLS
-            for v in range(2):
+            for v in v_parts:
                 for c in range(COLS // width):
                     piece = (slice(0, P), slice(2 * v, 2 * v + 2), slice(width * c, width * (c + 1)))
                     nc.sync.dma_start(out=x_rows[piece], in_=rows[piece])
-            return x_rows
 
-        def load_weight(words_in, scales_in, label):
-            words = consts.tile([P, HALVES, WIDTH], U32, name=label + "_words", align_bytes=64)
+        def load_planes(scales_in, label):
             planes = consts.tile([P, HALVES, WIDTH], U8, name=label + "_planes", align_bytes=64)
             nc.vector.memset(planes[:].bitcast(I32), 0)
             for quadrant in range(4):
@@ -76,18 +76,26 @@ def tile_selfprojection_pa_kernel(
                     .rearrange("g r n -> r g n")
                     .bitcast(I32),
                 )
+            return planes
+
+        def load_words(words_in, label):
+            words = consts.tile([P, HALVES, WIDTH], U32, name=label + "_words", align_bytes=64)
             nc.sync.dma_start(
                 out=words[:].bitcast(I32),
                 in_=words_in.rearrange("g p n t -> p g (n t)").bitcast(I32),
             )
-            return words, planes
+            return words
 
-        x_rows_of = {0: load_x(0)}
-        wj_words, wj_planes = load_weight(xj_words, xj_scales, "wj")
-        x_rows_of[1] = load_x(1)
-        x_rows_of[2] = load_x(2)
-        wi_words, wi_planes = load_weight(xi_words, xi_scales, "wi")
-        x_rows_of[3] = load_x(3)
+        x_rows_of = {}
+        load_x(0)
+        load_x(1, (0,))
+        wj_planes = load_planes(xj_scales, "wj")
+        wj_words = load_words(xj_words, "wj")
+        load_x(1, (1,))
+        load_x(2)
+        wi_planes = load_planes(xi_scales, "wi")
+        wi_words = load_words(xi_words, "wi")
+        load_x(3)
 
         identity = consts.tile([P, P], F32)
         make_identity(nc, identity[:])
@@ -114,20 +122,31 @@ def tile_selfprojection_pa_kernel(
             out=beta_sum_one[0:BATCH], in0=beta_sum[0:BATCH], scalar1=1.0, scalar2=None, op0=ALU.add
         )
 
-        def transpose_x(step, v, x_grouped):
+        def sort_x(step):
+            x_sorted = work.tile([P, 2, X_PASSES, 2, P], F32, name="x_sorted", bufs=4)
+            for v in range(2):
+                words = x_rows_of[step][:, 2 * v, :].bitcast(F32)
+                nc.vector.tensor_copy(
+                    out=x_sorted[:, v], in_=words.rearrange("p (c q u) -> p c u q", c=X_PASSES, u=2)
+                )
+            return x_sorted
+
+        def transpose_x(step, v, x_grouped, x_sorted=None):
             x_rows = x_rows_of[step]
             for c in range(X_PASSES):
                 xt_bank = ring.tile([P, 2, 2 * P], F32, tag="ring")
                 for e in range(2):
                     words = x_rows[:, 2 * v + e, :].bitcast(F32)
                     for u in range(2):
+                        if e == 0 and x_sorted is not None:
+                            columns = x_sorted[:, v, c, u, :]
+                        else:
+                            columns = words[:, 256 * c + u : 256 * (c + 1) : 2]
                         nc.tensor.transpose(
-                            out=xt_bank[:, u, P * e : P * (e + 1)],
-                            in_=words[:, 256 * c + u : 256 * (c + 1) : 2],
-                            identity=identity[:],
+                            out=xt_bank[:, u, P * e : P * (e + 1)], in_=columns, identity=identity[:]
                         )
                 grouped_words = x_grouped[:, c, 2 * P * v : 2 * P * (v + 1), :].bitcast(F32)
-                copy = nc.vector.tensor_copy if step == 0 and c == 1 else nc.scalar.copy
+                copy = nc.vector.tensor_copy if step <= 3 and c == 1 else nc.scalar.copy
                 copy(
                     out=grouped_words.rearrange("q (p e) u -> q p e u", e=2),
                     in_=xt_bank[:].rearrange("q u (e p) -> q p e u", e=2),
@@ -315,13 +334,17 @@ def tile_selfprojection_pa_kernel(
         quantised_x = {0: quantise_x(x_grouped)}
         y_columns_of = {}
         y_operand_of = {}
+        sorted_of = {}
         z_banks = []
         gained = []
         for b in range(BATCH):
             first, second = HALVES * b, HALVES * b + 1
             for step in (first + PREFETCH, second + PREFETCH):
                 if step < STEPS:
-                    x_rows_of[step] = load_x(step)
+                    load_x(step)
+            for step in (second + 1, second + 2):
+                if step < STEPS:
+                    sorted_of[step] = sort_x(step)
             y_operand_of[b] = new_y_operand()
             for half in range(HALVES):
                 step = HALVES * b + half
@@ -333,14 +356,15 @@ def tile_selfprojection_pa_kernel(
                     x_grouped = new_x_grouped()
                 for part in range(2):
                     if step + 1 < STEPS:
-                        transpose_x(step + 1, part, x_grouped)
+                        transpose_x(step + 1, part, x_grouped, sorted_of.get(step + 1))
                     if half == 0 and b >= 1:
                         transpose_y(1, part, y_columns_of[first - 1], y_operand_of[b - 1][0])
                     if half == 1:
                         transpose_y(0, part, y_columns_of[first], y_operand_of[b][0])
                     first_matmul(step, (2 * part, 2 * part + 1), *quantised_x[step], y_columns_of[step])
                     if half == 1 and b >= 1:
-                        second_matmuls((2 * part, 2 * part + 1), y_operand_of[b - 1], z_banks)
+                        z_tiles = (2 * part, 2 * part + 1) if b < last else range(I_TILES * part)
+                        second_matmuls(z_tiles, y_operand_of[b - 1], z_banks)
                     if half == 0 and part == 0 and b >= 2:
                         moments = row_moments(stats)
                         totals = ring.tile([P, 2], F32, tag="ring")
@@ -361,7 +385,7 @@ def tile_selfprojection_pa_kernel(
                             inv_std = inverse(std, P)
                             divide_by_std_and_bias(b - 2, 0, gained[0], inv_std)
                             divide_by_std_and_bias(b - 2, 1, gained[1], inv_std)
-                        if b >= 1:
+                        if 1 <= b < last:
                             all_row_statistics((0, 1), z_banks, stats)
                     if half == 1 and part == 1:
                         if b >= 2:
@@ -371,7 +395,7 @@ def tile_selfprojection_pa_kernel(
                             quantised_x[step + 1] = quantise_x(x_grouped)
                         quantise_y(0, *y_operand_of[b])
                         if b >= 1:
-                            all_row_statistics((2, 3), z_banks, stats)
+                            all_row_statistics((2, 3) if b < last else range(I_TILES), z_banks, stats)
 
         moments = row_moments(stats)
         for part in range(2):

@@ -101,6 +101,8 @@ def tile_selfprojection_pa_kernel(
         make_identity(nc, identity[:])
         averager = consts.tile([P, P], F32)
         nc.gpsimd.memset(averager[:], 1.0 / P)
+        half_averager = consts.tile([P, P], F32)
+        nc.gpsimd.memset(half_averager[:], 0.5 / P)
         one = consts.tile([P, 1], F32)
         nc.vector.memset(one[:], 1.0)
         warm = consts.tile([P, 1], F32)
@@ -223,6 +225,31 @@ def tile_selfprojection_pa_kernel(
         def row_statistics(i, z_bank, stats):
             nc.vector.bn_stats(out=stats[:, i, :], in_=z_bank[:])
 
+        def scalar_sums(i, z_bank, sums):
+            copied = work.tile([P, WIDTH], BF16)
+            nc.scalar.activation(
+                out=copied[:], in_=z_bank[:], func=ACT.Copy, accum_out=sums[:, 0, i : i + 1]
+            )
+            squares = work.tile([P, WIDTH], BF16)
+            nc.scalar.activation(
+                out=squares[:], in_=z_bank[:], func=ACT.Square, accum_out=sums[:, 1, i : i + 1]
+            )
+
+        def joined_moments(stats, sums):
+            two_tiles = row_moments(stats)
+            added = small.tile([P, 2], F32)
+            nc.vector.tensor_tensor(out=added[:], in0=sums[:, :, 0], in1=sums[:, :, 1], op=ALU.add)
+            moments = small.tile([P, 2], F32, name="joined")
+            nc.vector.scalar_tensor_tensor(
+                out=moments[:],
+                in0=added[:],
+                scalar=1.0 / (2 * WIDTH),
+                in1=two_tiles[:],
+                op0=ALU.mult,
+                op1=ALU.add,
+            )
+            return moments
+
         def row_moments(stats):
             moments = small.tile([P, 2], F32)
             nc.vector.bn_aggr(out=moments[:], in_=stats[:].rearrange("p i s -> p (i s)"))
@@ -236,8 +263,8 @@ def tile_selfprojection_pa_kernel(
             )
             return moments
 
-        def total_moments(moments, totals):
-            nc.tensor.matmul(out=totals[:], lhsT=averager[:], rhs=moments[:], start=True, stop=True)
+        def total_moments(moments, totals, weights):
+            nc.tensor.matmul(out=totals[:], lhsT=weights[:], rhs=moments[:], start=True, stop=True)
 
         def unbiased_variance(neg_variance, count, rows):
             unbiased = small.tile([P, 1], F32)
@@ -294,7 +321,7 @@ def tile_selfprojection_pa_kernel(
             return gained
 
         def divide_by_std_and_bias(b, i, gained, inv_std):
-            result = work.tile([P, WIDTH], F32, bufs=6)
+            result = work.tile([P, WIDTH], F32, bufs=8)
             nc.vector.scalar_tensor_tensor(
                 out=result[:],
                 in0=gained[:],
@@ -317,9 +344,8 @@ def tile_selfprojection_pa_kernel(
 
         def second_matmuls(i_tiles, y_operand, z_banks):
             for i in i_tiles:
-                z_bank = z_pool.tile([P, WIDTH], F32)
-                second_matmul(i, z_bank, y_operand[1], y_operand[2])
-                z_banks.append(z_bank)
+                z_banks.append(z_pool.tile([P, WIDTH], F32, name="z_bank"))
+                second_matmul(i, z_banks[i], y_operand[1], y_operand[2])
 
         def all_row_statistics(i_tiles, z_banks, stats):
             for i in i_tiles:
@@ -342,9 +368,6 @@ def tile_selfprojection_pa_kernel(
             for step in (first + PREFETCH, second + PREFETCH):
                 if step < STEPS:
                     load_x(step)
-            for step in (second + 1, second + 2):
-                if step < STEPS:
-                    sorted_of[step] = sort_x(step)
             y_operand_of[b] = new_y_operand()
             for half in range(HALVES):
                 step = HALVES * b + half
@@ -363,12 +386,14 @@ def tile_selfprojection_pa_kernel(
                         transpose_y(0, part, y_columns_of[first], y_operand_of[b][0])
                     first_matmul(step, (2 * part, 2 * part + 1), *quantised_x[step], y_columns_of[step])
                     if half == 1 and b >= 1:
-                        z_tiles = (2 * part, 2 * part + 1) if b < last else range(I_TILES * part)
+                        z_tiles = (2 * part, 2 * part + 1) if b < last else range(2 * part)
                         second_matmuls(z_tiles, y_operand_of[b - 1], z_banks)
+                    if part == 0 and step + 2 < STEPS:
+                        sorted_of[step + 2] = sort_x(step + 2)
                     if half == 0 and part == 0 and b >= 2:
                         moments = row_moments(stats)
                         totals = ring.tile([P, 2], F32, tag="ring")
-                        total_moments(moments, totals)
+                        total_moments(moments, totals, averager)
                         neg_mean, variance = mean_and_variance(totals)
                         gained = [subtract_mean_and_gain(i, z_banks[i], neg_mean) for i in (0, 1)]
                     if half == 0 and part == 1:
@@ -395,88 +420,106 @@ def tile_selfprojection_pa_kernel(
                             quantised_x[step + 1] = quantise_x(x_grouped)
                         quantise_y(0, *y_operand_of[b])
                         if b >= 1:
-                            all_row_statistics((2, 3) if b < last else range(I_TILES), z_banks, stats)
+                            all_row_statistics((2, 3) if b < last else (0, 1), z_banks, stats)
 
-        moments = row_moments(stats)
         for part in range(2):
             transpose_y(1, part, y_columns_of[STEPS - 1], y_operand_of[last][0])
-        nc.gpsimd.tensor_tensor(
+        nc.vector.tensor_tensor(
             out=c_columns[:, :, 0:BATCH],
             in0=c_parts[:, :, :, 0].rearrange("p b k -> p k b"),
             in1=c_parts[:, :, :, 1].rearrange("p b k -> p k b"),
             op=ALU.add,
         )
-        totals = ring.tile([P, 2], F32, tag="ring")
-        total_moments(moments, totals)
-        neg_mean, variance = mean_and_variance(totals)
-        gained = [subtract_mean_and_gain(i, z_banks[i], neg_mean) for i in (0, 1)]
-        std = square_root(variance, P)
-        quantise_y(1, *y_operand_of[last])
-        inv_std = inverse(std, P)
-        gained.extend([subtract_mean_and_gain(i, z_banks[i], neg_mean) for i in (2, 3)])
-        c_bank = ring.tile([P, J_BLOCKS, P], F32, tag="ring")
+        c_bank = ring.tile([P, WIDTH], F32, tag="ring")
         for jb in range(J_BLOCKS):
-            nc.tensor.transpose(out=c_bank[:, jb, :], in_=c_columns[:, jb, :], identity=identity[:])
-        c_rows = c_bank[0:BATCH].rearrange("b k j -> b (k j)")
-        for i in range(I_TILES):
-            scaled = work.tile([P, WIDTH], F32, bufs=4)
-            nc.scalar.activation(out=scaled[:], in_=gained[i][:], func=ACT.Copy, scale=inv_std[:])
-            result = work.tile([P, WIDTH], F32, bufs=6)
-            nc.gpsimd.tensor_tensor(out=result[:], in0=scaled[:], in1=beta[:, i, :], op=ALU.add)
-            nc.sync.dma_start(out=out[last - 1, P * i : P * (i + 1), :], in_=result[:])
-        z_banks = []
-        stats = small.tile([P, I_TILES, 6], F32)
-        second_matmuls(range(I_TILES), y_operand_of[last], z_banks)
-        c_stats = small.tile([P, 6], F32)
-        nc.vector.bn_stats(out=c_stats[0:BATCH], in_=c_rows)
-        c_moments = small.tile([P, 2], F32)
-        nc.vector.bn_aggr(out=c_moments[0:BATCH], in_=c_stats[0:BATCH])
+            nc.tensor.transpose(
+                out=c_bank[:, P * jb : P * (jb + 1)], in_=c_columns[:, jb, :], identity=identity[:]
+            )
+        quantise_y(1, *y_operand_of[last])
+        c_sums = small.tile([P, 2], F32)
+        c_copy = small.tile([P, WIDTH], F32)
+        nc.scalar.activation(
+            out=c_copy[0:BATCH], in_=c_bank[0:BATCH], func=ACT.Copy, accum_out=c_sums[0:BATCH, 0:1]
+        )
+        c_squares = small.tile([P, WIDTH], F32)
+        nc.scalar.activation(
+            out=c_squares[0:BATCH], in_=c_copy[0:BATCH], func=ACT.Square, accum_out=c_sums[0:BATCH, 1:2]
+        )
+        c_neg_mean = small.tile([P, 1], F32)
+        nc.vector.tensor_scalar(
+            out=c_neg_mean[0:BATCH], in0=c_sums[0:BATCH, 0:1], scalar1=-1.0 / WIDTH, scalar2=None, op0=ALU.mult
+        )
+        c_deviations = small.tile([P, 1], F32)
+        nc.vector.scalar_tensor_tensor(
+            out=c_deviations[0:BATCH],
+            in0=c_sums[0:BATCH, 0:1],
+            scalar=c_neg_mean[0:BATCH],
+            in1=c_sums[0:BATCH, 1:2],
+            op0=ALU.mult,
+            op1=ALU.add,
+        )
         c_variance = small.tile([P, 1], F32)
         nc.vector.tensor_scalar(
             out=c_variance[0:BATCH],
-            in0=c_moments[0:BATCH, 1:2],
-            scalar1=WIDTH / (WIDTH - 1),
-            scalar2=None,
+            in0=c_deviations[0:BATCH],
+            scalar1=1.0 / (WIDTH - 1),
+            scalar2=0.0,
             op0=ALU.mult,
+            op1=ALU.max,
         )
         c_std = square_root(c_variance, BATCH)
-        all_row_statistics((0, 1, 2, 3), z_banks, stats)
         c_inv_std = inverse(c_std, BATCH)
         c_shift = small.tile([P, 1], F32)
-        nc.vector.scalar_tensor_tensor(
-            out=c_shift[0:BATCH],
-            in0=c_moments[0:BATCH, 0:1],
-            scalar=-1.0,
-            in1=c_inv_std[0:BATCH],
-            op0=ALU.mult,
-            op1=ALU.mult,
+        nc.vector.tensor_tensor(
+            out=c_shift[0:BATCH], in0=c_neg_mean[0:BATCH], in1=c_inv_std[0:BATCH], op=ALU.mult
         )
         c_normal = small.tile([P, WIDTH], F32)
         nc.scalar.activation(
             out=c_normal[0:BATCH],
-            in_=c_rows,
+            in_=c_copy[0:BATCH],
             func=ACT.Identity,
             scale=c_inv_std[0:BATCH],
             bias=c_shift[0:BATCH],
         )
-        moments = row_moments(stats)
-        totals = ring.tile([P, 2], F32, tag="ring")
-        total_moments(moments, totals)
-        neg_mean, variance = mean_and_variance(totals)
-        std = square_root(variance, P)
-        gained = [subtract_mean_and_gain(i, z_banks[i], neg_mean) for i in (0, 1)]
-        inv_std = inverse(std, P)
-        divide_by_std_and_bias(last, 0, gained[0], inv_std)
-        divide_by_std_and_bias(last, 1, gained[1], inv_std)
-        for i in (2, 3):
-            gained.append(subtract_mean_and_gain(i, z_banks[i], neg_mean))
-            divide_by_std_and_bias(last, i, gained[i], inv_std)
         c_scaled = small.tile([P, WIDTH], F32)
-        nc.gpsimd.tensor_tensor(
+        nc.vector.tensor_tensor(
             out=c_scaled[0:BATCH], in0=c_normal[0:BATCH], in1=gamma_sum[0:BATCH], op=ALU.mult
         )
         c_result = small.tile([P, WIDTH], F32)
-        nc.gpsimd.tensor_tensor(
+        nc.vector.tensor_tensor(
             out=c_result[0:BATCH], in0=c_scaled[0:BATCH], in1=beta_sum_one[0:BATCH], op=ALU.add
         )
-        nc.gpsimd.dma_start(out=o_sum[:, :], in_=c_result[0:BATCH])
+        nc.sync.dma_start(out=o_sum[:, :], in_=c_result[0:BATCH])
+        second_matmuls((2, 3), y_operand_of[last - 1], z_banks)
+        all_row_statistics((2, 3), z_banks, stats)
+        moments = row_moments(stats)
+        last_z_banks = [ring.tile([P, WIDTH], F32, tag="ring", name="last_z_bank") for i in range(I_TILES)]
+        last_stats = small.tile([P, I_TILES, 6], F32, name="stats")
+        second_matmul(0, last_z_banks[0], *y_operand_of[last][1:])
+        second_matmul(1, last_z_banks[1], *y_operand_of[last][1:])
+        total_moments(moments, last_z_banks[3][:, 0:2], averager)
+        neg_mean, variance = mean_and_variance(last_z_banks[3][:, 0:2])
+        gained = [subtract_mean_and_gain(0, z_banks[0], neg_mean)]
+        second_matmul(2, last_z_banks[2], *y_operand_of[last][1:])
+        second_matmul(3, last_z_banks[3], *y_operand_of[last][1:])
+        all_row_statistics((0, 1), last_z_banks, last_stats)
+        last_sums = small.tile([P, 2, 2], F32, name="sums")
+        for i in (2, 3):
+            scalar_sums(i - 2, last_z_banks[i], last_sums)
+        last_moments = joined_moments(last_stats[:, 0:2, :], last_sums)
+        std = square_root(variance, P)
+        inv_std = inverse(std, P)
+        gained.extend([subtract_mean_and_gain(i, z_banks[i], neg_mean) for i in (1, 2, 3)])
+        totals = z_pool.tile([P, WIDTH], F32, name="z_bank")
+        total_moments(last_moments, totals[:, 0:2], half_averager)
+        last_neg_mean, last_variance = mean_and_variance(totals[:, 0:2])
+        last_std = square_root(last_variance, P)
+        for i in range(I_TILES):
+            divide_by_std_and_bias(last - 1, i, gained[i], inv_std)
+        last_gained = [subtract_mean_and_gain(i, last_z_banks[i], last_neg_mean) for i in (0, 1)]
+        last_inv_std = inverse(last_std, P)
+        divide_by_std_and_bias(last, 0, last_gained[0], last_inv_std)
+        divide_by_std_and_bias(last, 1, last_gained[1], last_inv_std)
+        for i in (2, 3):
+            last_gained.append(subtract_mean_and_gain(i, last_z_banks[i], last_neg_mean))
+            divide_by_std_and_bias(last, i, last_gained[i], last_inv_std)

@@ -54,17 +54,17 @@ def tile_selfprojection_pa_kernel(
         ring = stack.enter_context(tc.psum_pool(name="ring", bufs=4))
         z_pool = stack.enter_context(tc.psum_pool(name="z_pool", bufs=I_TILES))
 
-        def load_x(step, v_parts=(0, 1)):
+        def load_x(step, s_parts=(0, 1)):
             b, half = divmod(step, HALVES)
             if step not in x_rows_of:
                 x_rows_of[step] = x_pool.tile([P, PACK, COLS], BF16, name="x_rows")
             x_rows = x_rows_of[step]
-            rows = x[b, K_PASS * half : K_PASS * (half + 1), :].rearrange("(p t) n -> p t n", t=PACK)
+            rows = x[b, K_PASS * half : K_PASS * (half + 1), :].rearrange("(s p v) n -> p s v n", s=2, v=2)
             width = K_PASS if step == 0 else COLS
-            for v in v_parts:
+            for s in s_parts:
                 for c in range(COLS // width):
-                    piece = (slice(0, P), slice(2 * v, 2 * v + 2), slice(width * c, width * (c + 1)))
-                    nc.sync.dma_start(out=x_rows[piece], in_=rows[piece])
+                    cols = slice(width * c, width * (c + 1))
+                    nc.sync.dma_start(out=x_rows[:, 2 * s : 2 * s + 2, cols], in_=rows[:, s, :, cols])
 
         def load_planes(scales_in, label):
             planes = consts.tile([P, HALVES, WIDTH], U8, name=label + "_planes", align_bytes=64)
@@ -94,7 +94,8 @@ def tile_selfprojection_pa_kernel(
         load_x(1, (1,))
         load_x(2)
         wi_planes = load_planes(xi_scales, "wi")
-        wi_words = load_words(xi_words, "wi")
+        wi_words_as_stored = load_words(xi_words, "wi")
+        wi_words = consts.tile([P, HALVES, WIDTH], U32, name="wi_swapped", align_bytes=64)
         load_x(3)
 
         identity = consts.tile([P, P], F32)
@@ -124,34 +125,40 @@ def tile_selfprojection_pa_kernel(
             out=beta_sum_one[0:BATCH], in0=beta_sum[0:BATCH], scalar1=1.0, scalar2=None, op0=ALU.add
         )
 
+        def swap_middle_bytes(swapped, stored):
+            nc.vector.tensor_copy(out=swapped[:].bitcast(I32), in_=stored[:].bitcast(I32))
+            new_bytes = swapped[:].rearrange("p h i -> p (h i)").bitcast(U8).rearrange("p (w t) -> p w t", t=PACK)
+            old_bytes = stored[:].rearrange("p h i -> p (h i)").bitcast(U8).rearrange("p (w t) -> p w t", t=PACK)
+            for new, old in ((1, 2), (2, 1)):
+                nc.vector.tensor_copy(out=new_bytes[:, :, new], in_=old_bytes[:, :, old])
+
         def sort_x(step):
             x_sorted = work.tile([P, 2, X_PASSES, 2, P], F32, name="x_sorted", bufs=4)
-            for v in range(2):
-                words = x_rows_of[step][:, 2 * v, :].bitcast(F32)
+            for s in range(2):
+                words = x_rows_of[step][:, 2 * s, :].bitcast(F32)
                 nc.vector.tensor_copy(
-                    out=x_sorted[:, v], in_=words.rearrange("p (c q u) -> p c u q", c=X_PASSES, u=2)
+                    out=x_sorted[:, s], in_=words.rearrange("p (c q u) -> p c u q", c=X_PASSES, u=2)
                 )
             return x_sorted
 
-        def transpose_x(step, v, x_grouped, x_sorted=None):
+        def transpose_x(step, s, x_grouped, x_sorted=None):
             x_rows = x_rows_of[step]
             for c in range(X_PASSES):
                 xt_bank = ring.tile([P, 2, 2 * P], F32, tag="ring")
-                for e in range(2):
-                    words = x_rows[:, 2 * v + e, :].bitcast(F32)
+                for v in range(2):
+                    words = x_rows[:, 2 * s + v, :].bitcast(F32)
                     for u in range(2):
-                        if e == 0 and x_sorted is not None:
-                            columns = x_sorted[:, v, c, u, :]
+                        if v == 0 and x_sorted is not None:
+                            columns = x_sorted[:, s, c, u, :]
                         else:
                             columns = words[:, 256 * c + u : 256 * (c + 1) : 2]
                         nc.tensor.transpose(
-                            out=xt_bank[:, u, P * e : P * (e + 1)], in_=columns, identity=identity[:]
+                            out=xt_bank[:, u, P * v : P * (v + 1)], in_=columns, identity=identity[:]
                         )
-                grouped_words = x_grouped[:, c, 2 * P * v : 2 * P * (v + 1), :].bitcast(F32)
+                grouped_words = x_grouped[:, c].bitcast(F32).rearrange("q (v s p) u -> q v s p u", v=2, s=2)
                 copy = nc.vector.tensor_copy if step <= 3 and c == 1 else nc.scalar.copy
                 copy(
-                    out=grouped_words.rearrange("q (p e) u -> q p e u", e=2),
-                    in_=xt_bank[:].rearrange("q u (e p) -> q p e u", e=2),
+                    out=grouped_words[:, :, s], in_=xt_bank[:].rearrange("q u (v p) -> q v p u", v=2)
                 )
 
         def quantise_x(x_grouped, calls=1):
@@ -388,8 +395,10 @@ def tile_selfprojection_pa_kernel(
                     if half == 1 and b >= 1:
                         z_tiles = (2 * part, 2 * part + 1) if b < last else range(2 * part)
                         second_matmuls(z_tiles, y_operand_of[b - 1], z_banks)
-                    if part == 0 and step + 2 < STEPS:
+                    if part == 0 and 1 <= step < STEPS - 2:
                         sorted_of[step + 2] = sort_x(step + 2)
+                    if step == 1 and part == 1:
+                        swap_middle_bytes(wi_words, wi_words_as_stored)
                     if half == 0 and part == 0 and b >= 2:
                         moments = row_moments(stats)
                         totals = ring.tile([P, 2], F32, tag="ring")

@@ -61,9 +61,9 @@ def tile_selfprojection_pa_kernel(
             x_rows = x_rows_of[step]
             rows = x[b, K_PASS * half : K_PASS * (half + 1), :].rearrange("(s p v) n -> p s v n", s=2, v=2)
             width = K_PASS if step == 0 else COLS
-            for s in s_parts:
-                for c in range(COLS // width):
-                    cols = slice(width * c, width * (c + 1))
+            for c in range(COLS // width):
+                cols = slice(width * c, width * (c + 1))
+                for s in s_parts:
                     nc.sync.dma_start(out=x_rows[:, 2 * s : 2 * s + 2, cols], in_=rows[:, s, :, cols])
 
         def load_planes(scales_in, label):
@@ -141,9 +141,9 @@ def tile_selfprojection_pa_kernel(
                 )
             return x_sorted
 
-        def transpose_x(step, s, x_grouped, x_sorted=None):
+        def transpose_x(step, s, x_grouped, x_sorted=None, passes=range(X_PASSES)):
             x_rows = x_rows_of[step]
-            for c in range(X_PASSES):
+            for c in passes:
                 xt_bank = ring.tile([P, 2, 2 * P], F32, tag="ring")
                 for v in range(2):
                     words = x_rows[:, 2 * s + v, :].bitcast(F32)
@@ -156,7 +156,8 @@ def tile_selfprojection_pa_kernel(
                             out=xt_bank[:, u, P * v : P * (v + 1)], in_=columns, identity=identity[:]
                         )
                 grouped_words = x_grouped[:, c].bitcast(F32).rearrange("q (v s p) u -> q v s p u", v=2, s=2)
-                copy = nc.vector.tensor_copy if step <= 3 and c == 1 else nc.scalar.copy
+                on_vector = s == 1 if step == 0 else step <= 3 and c == 1
+                copy = nc.vector.tensor_copy if on_vector else nc.scalar.copy
                 copy(
                     out=grouped_words[:, :, s], in_=xt_bank[:].rearrange("q u (v p) -> q v p u", v=2)
                 )
@@ -362,9 +363,10 @@ def tile_selfprojection_pa_kernel(
             return work.tile([P, X_PASSES, K_PASS, PACK], BF16, name="x_grouped", align_bytes=64)
 
         x_grouped = new_x_grouped()
-        for v in range(2):
-            transpose_x(0, v, x_grouped)
-        quantised_x = {0: quantise_x(x_grouped)}
+        for c in range(X_PASSES):
+            for s in range(2):
+                transpose_x(0, s, x_grouped, passes=(c,))
+        quantised_x = {0: quantise_x(x_grouped, calls=X_PASSES)}
         y_columns_of = {}
         y_operand_of = {}
         sorted_of = {}
@@ -406,6 +408,7 @@ def tile_selfprojection_pa_kernel(
                         neg_mean, variance = mean_and_variance(totals)
                         gained = [subtract_mean_and_gain(i, z_banks[i], neg_mean) for i in (0, 1)]
                     if half == 0 and part == 1:
+                        quantised_x[step + 1] = quantise_x(x_grouped)
                         if b >= 1:
                             quantise_y(1, *y_operand_of[b - 1])
                         if b >= 2:
@@ -413,7 +416,6 @@ def tile_selfprojection_pa_kernel(
                                 [subtract_mean_and_gain(i, z_banks[i], neg_mean) for i in (2, 3)]
                             )
                             std = square_root(variance, P)
-                        quantised_x[step + 1] = quantise_x(x_grouped)
                     if half == 1 and part == 0:
                         if b >= 2:
                             inv_std = inverse(std, P)
@@ -422,12 +424,12 @@ def tile_selfprojection_pa_kernel(
                         if 1 <= b < last:
                             all_row_statistics((0, 1), z_banks, stats)
                     if half == 1 and part == 1:
-                        if b >= 2:
-                            divide_by_std_and_bias(b - 2, 2, gained[2], inv_std)
-                            divide_by_std_and_bias(b - 2, 3, gained[3], inv_std)
                         if step + 1 < STEPS:
                             quantised_x[step + 1] = quantise_x(x_grouped)
                         quantise_y(0, *y_operand_of[b])
+                        if b >= 2:
+                            divide_by_std_and_bias(b - 2, 2, gained[2], inv_std)
+                            divide_by_std_and_bias(b - 2, 3, gained[3], inv_std)
                         if b >= 1:
                             all_row_statistics((2, 3) if b < last else (0, 1), z_banks, stats)
 

@@ -54,17 +54,17 @@ def tile_selfprojection_pa_kernel(
         ring = stack.enter_context(tc.psum_pool(name="ring", bufs=4))
         z_pool = stack.enter_context(tc.psum_pool(name="z_pool", bufs=I_TILES))
 
-        def load_x(step, s_parts=(0, 1)):
+        def load_x(step, v_parts=(0, 1)):
             b, half = divmod(step, HALVES)
             if step not in x_rows_of:
                 x_rows_of[step] = x_pool.tile([P, PACK, COLS], BF16, name="x_rows")
             x_rows = x_rows_of[step]
-            rows = x[b, K_PASS * half : K_PASS * (half + 1), :].rearrange("(s p v) n -> p s v n", s=2, v=2)
+            rows = x[b, K_PASS * half : K_PASS * (half + 1), :].rearrange("(p t) n -> p t n", t=PACK)
             width = K_PASS if step == 0 else COLS
             for c in range(COLS // width):
-                cols = slice(width * c, width * (c + 1))
-                for s in s_parts:
-                    nc.sync.dma_start(out=x_rows[:, 2 * s : 2 * s + 2, cols], in_=rows[:, s, :, cols])
+                for v in v_parts:
+                    piece = (slice(0, P), slice(2 * v, 2 * v + 2), slice(width * c, width * (c + 1)))
+                    nc.sync.dma_start(out=x_rows[piece], in_=rows[piece])
 
         def load_planes(scales_in, label):
             planes = consts.tile([P, HALVES, WIDTH], U8, name=label + "_planes", align_bytes=64)
@@ -94,8 +94,7 @@ def tile_selfprojection_pa_kernel(
         load_x(1, (1,))
         load_x(2)
         wi_planes = load_planes(xi_scales, "wi")
-        wi_words_as_stored = load_words(xi_words, "wi")
-        wi_words = consts.tile([P, HALVES, WIDTH], U32, name="wi_swapped", align_bytes=64)
+        wi_words = load_words(xi_words, "wi")
         load_x(3)
 
         identity = consts.tile([P, P], F32)
@@ -125,41 +124,35 @@ def tile_selfprojection_pa_kernel(
             out=beta_sum_one[0:BATCH], in0=beta_sum[0:BATCH], scalar1=1.0, scalar2=None, op0=ALU.add
         )
 
-        def swap_middle_bytes(swapped, stored):
-            nc.vector.tensor_copy(out=swapped[:].bitcast(I32), in_=stored[:].bitcast(I32))
-            new_bytes = swapped[:].rearrange("p h i -> p (h i)").bitcast(U8).rearrange("p (w t) -> p w t", t=PACK)
-            old_bytes = stored[:].rearrange("p h i -> p (h i)").bitcast(U8).rearrange("p (w t) -> p w t", t=PACK)
-            for new, old in ((1, 2), (2, 1)):
-                nc.vector.tensor_copy(out=new_bytes[:, :, new], in_=old_bytes[:, :, old])
-
         def sort_x(step):
             x_sorted = work.tile([P, 2, X_PASSES, 2, P], F32, name="x_sorted", bufs=4)
-            for s in range(2):
-                words = x_rows_of[step][:, 2 * s, :].bitcast(F32)
+            for v in range(2):
+                words = x_rows_of[step][:, 2 * v, :].bitcast(F32)
                 nc.vector.tensor_copy(
-                    out=x_sorted[:, s], in_=words.rearrange("p (c q u) -> p c u q", c=X_PASSES, u=2)
+                    out=x_sorted[:, v], in_=words.rearrange("p (c q u) -> p c u q", c=X_PASSES, u=2)
                 )
             return x_sorted
 
-        def transpose_x(step, s, x_grouped, x_sorted=None, passes=range(X_PASSES)):
+        def transpose_x(step, v, x_grouped, x_sorted=None, passes=range(X_PASSES)):
             x_rows = x_rows_of[step]
             for c in passes:
                 xt_bank = ring.tile([P, 2, 2 * P], F32, tag="ring")
-                for v in range(2):
-                    words = x_rows[:, 2 * s + v, :].bitcast(F32)
+                for e in range(2):
+                    words = x_rows[:, 2 * v + e, :].bitcast(F32)
                     for u in range(2):
-                        if v == 0 and x_sorted is not None:
-                            columns = x_sorted[:, s, c, u, :]
+                        if e == 0 and x_sorted is not None:
+                            columns = x_sorted[:, v, c, u, :]
                         else:
                             columns = words[:, 256 * c + u : 256 * (c + 1) : 2]
                         nc.tensor.transpose(
-                            out=xt_bank[:, u, P * v : P * (v + 1)], in_=columns, identity=identity[:]
+                            out=xt_bank[:, u, P * e : P * (e + 1)], in_=columns, identity=identity[:]
                         )
-                grouped_words = x_grouped[:, c].bitcast(F32).rearrange("q (v s p) u -> q v s p u", v=2, s=2)
-                on_vector = s == 1 if step == 0 else step <= 3 and c == 1
+                grouped_words = x_grouped[:, c, 2 * P * v : 2 * P * (v + 1), :].bitcast(F32)
+                on_vector = v == 1 if step == 0 else step <= 3 and c == 1
                 copy = nc.vector.tensor_copy if on_vector else nc.scalar.copy
                 copy(
-                    out=grouped_words[:, :, s], in_=xt_bank[:].rearrange("q u (v p) -> q v p u", v=2)
+                    out=grouped_words.rearrange("q (p e) u -> q p e u", e=2),
+                    in_=xt_bank[:].rearrange("q u (e p) -> q p e u", e=2),
                 )
 
         def quantise_x(x_grouped, calls=1):
@@ -364,8 +357,8 @@ def tile_selfprojection_pa_kernel(
 
         x_grouped = new_x_grouped()
         for c in range(X_PASSES):
-            for s in range(2):
-                transpose_x(0, s, x_grouped, passes=(c,))
+            for v in range(2):
+                transpose_x(0, v, x_grouped, passes=(c,))
         quantised_x = {0: quantise_x(x_grouped, calls=X_PASSES)}
         y_columns_of = {}
         y_operand_of = {}
@@ -393,14 +386,13 @@ def tile_selfprojection_pa_kernel(
                         transpose_y(1, part, y_columns_of[first - 1], y_operand_of[b - 1][0])
                     if half == 1:
                         transpose_y(0, part, y_columns_of[first], y_operand_of[b][0])
+                    if half == 1 and 1 <= b < last:
+                        second_matmuls((2 * part, 2 * part + 1), y_operand_of[b - 1], z_banks)
                     first_matmul(step, (2 * part, 2 * part + 1), *quantised_x[step], y_columns_of[step])
-                    if half == 1 and b >= 1:
-                        z_tiles = (2 * part, 2 * part + 1) if b < last else range(2 * part)
-                        second_matmuls(z_tiles, y_operand_of[b - 1], z_banks)
+                    if half == 1 and b == last:
+                        second_matmuls(range(2 * part), y_operand_of[b - 1], z_banks)
                     if part == 0 and 1 <= step < STEPS - 2:
                         sorted_of[step + 2] = sort_x(step + 2)
-                    if step == 1 and part == 1:
-                        swap_middle_bytes(wi_words, wi_words_as_stored)
                     if half == 0 and part == 0 and b >= 2:
                         moments = row_moments(stats)
                         totals = ring.tile([P, 2], F32, tag="ring")

from contextlib import ExitStack

import concourse.mybir as mybir
from concourse.masks import make_identity

F32 = mybir.dt.float32
BF16 = mybir.dt.bfloat16
I32 = mybir.dt.int32
U32 = mybir.dt.uint32
U8 = mybir.dt.uint8
FP8X4 = mybir.dt.float8_e4m3fn_x4
ALU = mybir.AluOpType
ACT = mybir.ActivationFunctionType
AXIS = mybir.AxisListType

P = 128
PACK = 4
K_PASS = P * PACK
BATCH = 6
ROWS = 1024
COLS = 1024
WIDTH = 512
X_PASSES = COLS // K_PASS
HALVES = ROWS // K_PASS
STEPS = BATCH * HALVES
J_BLOCKS = WIDTH // P
I_TILES = WIDTH // P
EPS = 1e-5
PREFETCH = 4

FLOPS = 2 * BATCH * ROWS * COLS * WIDTH + 2 * BATCH * ROWS * WIDTH * WIDTH


def tile_selfprojection_pa_kernel(
    tc,
    x,
    xj_words,
    xj_scales,
    xi_words,
    xi_scales,
    gamma_o_sum,
    gamma_o,
    beta_o_sum,
    beta_o,
    out,
    o_sum,
):
    nc = tc.nc
    with ExitStack() as stack:
        consts = stack.enter_context(tc.tile_pool(name="consts", bufs=1))
        x_pool = stack.enter_context(tc.tile_pool(name="x_pool", bufs=PREFETCH + 1))
        work = stack.enter_context(tc.tile_pool(name="work", bufs=2))
        small = stack.enter_context(tc.tile_pool(name="small", bufs=3))
        ring = stack.enter_context(tc.psum_pool(name="ring", bufs=4))
        z_pool = stack.enter_context(tc.psum_pool(name="z_pool", bufs=I_TILES))

        def load_x(step, v_parts=(0, 1)):
            b, half = divmod(step, HALVES)
            if step not in x_rows_of:
                x_rows_of[step] = x_pool.tile([P, PACK, COLS], BF16, name="x_rows")
            x_rows = x_rows_of[step]
            rows = x[b, K_PASS * half : K_PASS * (half + 1), :].rearrange("(p t) n -> p t n", t=PACK)
            width = K_PASS if step == 0 else COLS
            for c in range(COLS // width):
                for v in v_parts:
                    piece = (slice(0, P), slice(2 * v, 2 * v + 2), slice(width * c, width * (c + 1)))
                    nc.sync.dma_start(out=x_rows[piece], in_=rows[piece])

        def load_planes(scales_in, label):
            planes = consts.tile([P, HALVES, WIDTH], U8, name=label + "_planes", align_bytes=64)
            nc.vector.memset(planes[:].bitcast(I32), 0)
            for quadrant in range(4):
                nc.sync.dma_start(
                    out=planes[32 * quadrant : 32 * quadrant + 4].bitcast(I32),
                    in_=scales_in[:, 4 * quadrant : 4 * quadrant + 4, :]
                    .rearrange("g r n -> r g n")
                    .bitcast(I32),
                )
            return planes

        def load_words(words_in, label):
            words = consts.tile([P, HALVES, WIDTH], U32, name=label + "_words", align_bytes=64)
            nc.sync.dma_start(
                out=words[:].bitcast(I32),
                in_=words_in.rearrange("g p n t -> p g (n t)").bitcast(I32),
            )
            return words

        x_rows_of = {}
        load_x(0)
        load_x(1, (0,))
        wj_planes = load_planes(xj_scales, "wj")
        wj_words = load_words(xj_words, "wj")
        load_x(1, (1,))
        load_x(2)
        wi_planes = load_planes(xi_scales, "wi")
        wi_words = load_words(xi_words, "wi")
        load_x(3)

        identity = consts.tile([P, P], F32)
        make_identity(nc, identity[:])
        averager = consts.tile([P, P], F32)
        nc.gpsimd.memset(averager[:], 1.0 / P)
        half_averager = consts.tile([P, P], F32)
        nc.gpsimd.memset(half_averager[:], 0.5 / P)
        one = consts.tile([P, 1], F32)
        nc.vector.memset(one[:], 1.0)
        warm = consts.tile([P, 1], F32)
        nc.scalar.activation(out=warm[:], in_=one[:], func=ACT.Sqrt)
        c_parts = consts.tile([P, BATCH, J_BLOCKS, HALVES], F32)
        c_columns = consts.tile([P, J_BLOCKS, P], F32)
        nc.gpsimd.memset(c_columns[:], 0.0)

        gamma = consts.tile([P, I_TILES, WIDTH], BF16)
        nc.sync.dma_start(out=gamma[:], in_=gamma_o.rearrange("(i p) j -> p i j", p=P))
        beta = consts.tile([P, I_TILES, WIDTH], BF16)
        nc.sync.dma_start(out=beta[:], in_=beta_o.rearrange("(i p) j -> p i j", p=P))
        gamma_sum = consts.tile([P, WIDTH], BF16)
        nc.sync.dma_start(out=gamma_sum[0:BATCH], in_=gamma_o_sum.partition_broadcast(BATCH))
        beta_sum = consts.tile([P, WIDTH], BF16)
        nc.sync.dma_start(out=beta_sum[0:BATCH], in_=beta_o_sum.partition_broadcast(BATCH))
        beta_sum_one = consts.tile([P, WIDTH], F32)
        nc.gpsimd.tensor_scalar(
            out=beta_sum_one[0:BATCH], in0=beta_sum[0:BATCH], scalar1=1.0, scalar2=None, op0=ALU.add
        )

        def sort_x(step):
            x_sorted = work.tile([P, 2, X_PASSES, 2, P], F32, name="x_sorted", bufs=4)
            for v in range(2):
                words = x_rows_of[step][:, 2 * v, :].bitcast(F32)
                nc.vector.tensor_copy(
                    out=x_sorted[:, v], in_=words.rearrange("p (c q u) -> p c u q", c=X_PASSES, u=2)
                )
            return x_sorted

        def transpose_x(step, v, x_grouped, x_sorted=None, passes=range(X_PASSES)):
            x_rows = x_rows_of[step]
            for c in passes:
                xt_bank = ring.tile([P, 2, 2 * P], F32, tag="ring")
                for e in range(2):
                    words = x_rows[:, 2 * v + e, :].bitcast(F32)
                    for u in range(2):
                        if e == 0 and x_sorted is not None:
                            columns = x_sorted[:, v, c, u, :]
                        else:
                            columns = words[:, 256 * c + u : 256 * (c + 1) : 2]
                        nc.tensor.transpose(
                            out=xt_bank[:, u, P * e : P * (e + 1)], in_=columns, identity=identity[:]
                        )
                grouped_words = x_grouped[:, c, 2 * P * v : 2 * P * (v + 1), :].bitcast(F32)
                on_vector = v == 1 if step == 0 else step <= 3 and c == 1
                copy = nc.vector.tensor_copy if on_vector else nc.scalar.copy
                copy(
                    out=grouped_words.rearrange("q (p e) u -> q p e u", e=2),
                    in_=xt_bank[:].rearrange("q u (e p) -> q p e u", e=2),
                )

        def quantise_x(x_grouped, calls=1):
            x_words = work.tile([P, X_PASSES, K_PASS], U32, align_bytes=64)
            x_planes = work.tile([P, X_PASSES, K_PASS], U8, align_bytes=64)
            passes = X_PASSES // calls
            for call in range(calls):
                some = slice(passes * call, passes * (call + 1))
                nc.vector.quantize_mx(
                    out=x_words[:, some, :].rearrange("q c m -> q (c m)").bitcast(FP8X4),
                    scales=x_planes[:, some, :].rearrange("q c m -> q (c m)"),
                    in_=x_grouped[:, some, :, :].rearrange("q c m t -> q (c m t)"),
                )
            return x_words, x_planes

        def first_matmul(step, j_blocks, x_words, x_planes, y_columns):
            b, half = divmod(step, HALVES)
            for jb in j_blocks:
                j_cols = slice(P * jb, P * (jb + 1))
                y_bank = ring.tile([P, K_PASS], F32, tag="ring")
                for c in range(X_PASSES):
                    nc.tensor.matmul_mx(
                        out=y_bank[:],
                        lhsT=wj_words[:, c, j_cols].bitcast(FP8X4),
                        lhsT_scale=wj_planes[:, c, j_cols],
                        rhs=x_words[:, c, :].bitcast(FP8X4),
                        rhs_scale=x_planes[:, c, :],
                        start=(c == 0),
                        stop=(c == X_PASSES - 1),
                    )
                nc.scalar.activation(
                    out=y_columns[:, jb, :],
                    in_=y_bank[:],
                    func=ACT.Copy,
                    accum_out=c_parts[:, b, jb, half : half + 1],
                )

        def transpose_y(half, pair, y_columns, y_grouped):
            yt_bank = ring.tile([P, 2, 2 * P], F32, tag="ring")
            for i in range(2):
                words = y_columns[:, 2 * pair + i, :].bitcast(F32)
                for v in range(2):
                    nc.tensor.transpose(
                        out=yt_bank[:, v, P * i : P * (i + 1)],
                        in_=words[:, P * v : P * (v + 1)],
                        identity=identity[:],
                    )
            grouped_words = y_grouped[:, half, 2 * P * pair : 2 * P * (pair + 1), :].bitcast(F32)
            nc.scalar.copy(out=grouped_words, in_=yt_bank[:].rearrange("p v j -> p j v"))

        def quantise_y(half, y_grouped, y_words, y_planes):
            nc.vector.quantize_mx(
                out=y_words[:, half, :].bitcast(FP8X4),
                scales=y_planes[:, half, :],
                in_=y_grouped[:, half, :, :].rearrange("p j t -> p (j t)"),
            )

        def second_matmul(i, z_bank, y_words, y_planes):
            i_cols = slice(P * i, P * (i + 1))
            for half in range(HALVES):
                nc.tensor.matmul_mx(
                    out=z_bank[:],
                    lhsT=wi_words[:, half, i_cols].bitcast(FP8X4),
                    lhsT_scale=wi_planes[:, half, i_cols],
                    rhs=y_words[:, half, :].bitcast(FP8X4),
                    rhs_scale=y_planes[:, half, :],
                    start=(half == 0),
                    stop=(half == HALVES - 1),
                )

        def row_statistics(i, z_bank, stats):
            nc.vector.bn_stats(out=stats[:, i, :], in_=z_bank[:])

        def scalar_sums(i, z_bank, sums):
            copied = work.tile([P, WIDTH], BF16)
            nc.scalar.activation(
                out=copied[:], in_=z_bank[:], func=ACT.Copy, accum_out=sums[:, 0, i : i + 1]
            )
            squares = work.tile([P, WIDTH], BF16)
            nc.scalar.activation(
                out=squares[:], in_=z_bank[:], func=ACT.Square, accum_out=sums[:, 1, i : i + 1]
            )

        def joined_moments(stats, sums):
            two_tiles = row_moments(stats)
            added = small.tile([P, 2], F32)
            nc.vector.tensor_tensor(out=added[:], in0=sums[:, :, 0], in1=sums[:, :, 1], op=ALU.add)
            moments = small.tile([P, 2], F32, name="joined")
            nc.vector.scalar_tensor_tensor(
                out=moments[:],
                in0=added[:],
                scalar=1.0 / (2 * WIDTH),
                in1=two_tiles[:],
                op0=ALU.mult,
                op1=ALU.add,
            )
            return moments

        def row_moments(stats):
            moments = small.tile([P, 2], F32)
            nc.vector.bn_aggr(out=moments[:], in_=stats[:].rearrange("p i s -> p (i s)"))
            nc.vector.scalar_tensor_tensor(
                out=moments[:, 1:2],
                in0=moments[:, 0:1],
                scalar=moments[:, 0:1],
                in1=moments[:, 1:2],
                op0=ALU.mult,
                op1=ALU.add,
            )
            return moments

        def total_moments(moments, totals, weights):
            nc.tensor.matmul(out=totals[:], lhsT=weights[:], rhs=moments[:], start=True, stop=True)

        def unbiased_variance(neg_variance, count, rows):
            unbiased = small.tile([P, 1], F32)
            nc.vector.tensor_scalar(
                out=unbiased[0:rows],
                in0=neg_variance,
                scalar1=-count / (count - 1),
                scalar2=0.0,
                op0=ALU.mult,
                op1=ALU.max,
            )
            return unbiased

        def square_root(variance, rows):
            std = small.tile([P, 1], F32)
            nc.scalar.activation(out=std[0:rows], in_=variance[0:rows], func=ACT.Sqrt)
            return std

        def inverse(std, rows):
            std_eps = small.tile([P, 1], F32)
            nc.vector.tensor_scalar(
                out=std_eps[0:rows], in0=std[0:rows], scalar1=EPS, scalar2=None, op0=ALU.add
            )
            inv_std = small.tile([P, 1], F32)
            nc.vector.reciprocal(out=inv_std[0:rows], in_=std_eps[0:rows])
            return inv_std

        def mean_and_variance(totals):
            neg_mean = small.tile([P, 1], F32)
            nc.vector.tensor_scalar(
                out=neg_mean[:], in0=totals[:, 0:1], scalar1=-1.0, scalar2=None, op0=ALU.mult
            )
            neg_variance = small.tile([P, 1], F32)
            nc.vector.scalar_tensor_tensor(
                out=neg_variance[:],
                in0=neg_mean[:],
                scalar=neg_mean[:],
                in1=totals[:, 1:2],
                op0=ALU.mult,
                op1=ALU.subtract,
            )
            return neg_mean, unbiased_variance(neg_variance[:], WIDTH * WIDTH, P)

        def subtract_mean_and_gain(i, z_bank, neg_mean):
            gained = work.tile([P, WIDTH], F32, bufs=8)
            nc.vector.scalar_tensor_tensor(
                out=gained[:],
                in0=z_bank[:],
                scalar=neg_mean[:],
                in1=gamma[:, i, :],
                op0=ALU.add,
                op1=ALU.mult,
            )
            return gained

        def divide_by_std_and_bias(b, i, gained, inv_std):
            result = work.tile([P, WIDTH], F32, bufs=8)
            nc.vector.scalar_tensor_tensor(
                out=result[:],
                in0=gained[:],
                scalar=inv_std[:],
                in1=beta[:, i, :],
                op0=ALU.mult,
                op1=ALU.add,
            )
            nc.sync.dma_start(out=out[b, P * i : P * (i + 1), :], in_=result[:])

        stack.enter_context(tc.manual_schedule(engines={mybir.EngineType.PE}))
        last = BATCH - 1

        def new_y_operand():
            return (
                work.tile([P, HALVES, WIDTH, PACK], BF16, name="y_grouped", align_bytes=64),
                work.tile([P, HALVES, WIDTH], U32, name="y_words", align_bytes=64),
                work.tile([P, HALVES, WIDTH], U8, name="y_planes", align_bytes=64),
            )

        def second_matmuls(i_tiles, y_operand, z_banks):
            for i in i_tiles:
                z_banks.append(z_pool.tile([P, WIDTH], F32, name="z_bank"))
                second_matmul(i, z_banks[i], y_operand[1], y_operand[2])

        def all_row_statistics(i_tiles, z_banks, stats):
            for i in i_tiles:
                row_statistics(i, z_banks[i], stats)

        def new_x_grouped():
            return work.tile([P, X_PASSES, K_PASS, PACK], BF16, name="x_grouped", align_bytes=64)

        x_grouped = new_x_grouped()
        for c in range(X_PASSES):
            for v in range(2):
                transpose_x(0, v, x_grouped, passes=(c,))
        quantised_x = {0: quantise_x(x_grouped, calls=X_PASSES)}
        y_columns_of = {}
        y_operand_of = {}
        sorted_of = {}
        z_banks = []
        gained = []
        for b in range(BATCH):
            first, second = HALVES * b, HALVES * b + 1
            for step in (first + PREFETCH, second + PREFETCH):
                if step < STEPS:
                    load_x(step)
            y_operand_of[b] = new_y_operand()
            for half in range(HALVES):
                step = HALVES * b + half
                y_columns_of[step] = work.tile([P, J_BLOCKS, K_PASS], BF16, name="y_columns", bufs=4)
                if half == 1 and b >= 1:
                    z_banks = []
                    stats = small.tile([P, I_TILES, 6], F32, name="stats")
                if step + 1 < STEPS:
                    x_grouped = new_x_grouped()
                for part in range(2):
                    if step + 1 < STEPS:
                        transpose_x(step + 1, part, x_grouped, sorted_of.get(step + 1))
                    if half == 0 and b >= 1:
                        transpose_y(1, part, y_columns_of[first - 1], y_operand_of[b - 1][0])
                    if half == 1:
                        transpose_y(0, part, y_columns_of[first], y_operand_of[b][0])
                    if half == 1 and 1 <= b < last:
                        second_matmuls((2 * part, 2 * part + 1), y_operand_of[b - 1], z_banks)
                    first_matmul(step, (2 * part, 2 * part + 1), *quantised_x[step], y_columns_of[step])
                    if half == 1 and b == last:
                        second_matmuls(range(2 * part), y_operand_of[b - 1], z_banks)
                    if part == 0 and 1 <= step < STEPS - 2:
                        sorted_of[step + 2] = sort_x(step + 2)
                    if half == 0 and part == 0 and b >= 2:
                        moments = row_moments(stats)
                        totals = ring.tile([P, 2], F32, tag="ring")
                        total_moments(moments, totals, averager)
                        neg_mean, variance = mean_and_variance(totals)
                        gained = [subtract_mean_and_gain(i, z_banks[i], neg_mean) for i in (0, 1)]
                    if half == 0 and part == 1:
                        quantised_x[step + 1] = quantise_x(x_grouped)
                        if b >= 1:
                            quantise_y(1, *y_operand_of[b - 1])
                        if b >= 2:
                            gained.extend(
                                [subtract_mean_and_gain(i, z_banks[i], neg_mean) for i in (2, 3)]
                            )
                            std = square_root(variance, P)
                    if half == 1 and part == 0:
                        if b >= 2:
                            inv_std = inverse(std, P)
                            divide_by_std_and_bias(b - 2, 0, gained[0], inv_std)
                            divide_by_std_and_bias(b - 2, 1, gained[1], inv_std)
                        if 1 <= b < last:
                            all_row_statistics((0, 1), z_banks, stats)
                    if half == 1 and part == 1:
                        if step + 1 < STEPS:
                            quantised_x[step + 1] = quantise_x(x_grouped)
                        quantise_y(0, *y_operand_of[b])
                        if b >= 2:
                            divide_by_std_and_bias(b - 2, 2, gained[2], inv_std)
                            divide_by_std_and_bias(b - 2, 3, gained[3], inv_std)
                        if b >= 1:
                            all_row_statistics((2, 3) if b < last else (0, 1), z_banks, stats)

        for part in range(2):
            transpose_y(1, part, y_columns_of[STEPS - 1], y_operand_of[last][0])
        nc.vector.tensor_tensor(
            out=c_columns[:, :, 0:BATCH],
            in0=c_parts[:, :, :, 0].rearrange("p b k -> p k b"),
            in1=c_parts[:, :, :, 1].rearrange("p b k -> p k b"),
            op=ALU.add,
        )
        c_bank = ring.tile([P, WIDTH], F32, tag="ring")
        for jb in range(J_BLOCKS):
            nc.tensor.transpose(
                out=c_bank[:, P * jb : P * (jb + 1)], in_=c_columns[:, jb, :], identity=identity[:]
            )
        quantise_y(1, *y_operand_of[last])
        c_sums = small.tile([P, 2], F32)
        c_copy = small.tile([P, WIDTH], F32)
        nc.scalar.activation(
            out=c_copy[0:BATCH], in_=c_bank[0:BATCH], func=ACT.Copy, accum_out=c_sums[0:BATCH, 0:1]
        )
        c_squares = small.tile([P, WIDTH], F32)
        nc.scalar.activation(
            out=c_squares[0:BATCH], in_=c_copy[0:BATCH], func=ACT.Square, accum_out=c_sums[0:BATCH, 1:2]
        )
        c_neg_mean = small.tile([P, 1], F32)
        nc.vector.tensor_scalar(
            out=c_neg_mean[0:BATCH], in0=c_sums[0:BATCH, 0:1], scalar1=-1.0 / WIDTH, scalar2=None, op0=ALU.mult
        )
        c_deviations = small.tile([P, 1], F32)
        nc.vector.scalar_tensor_tensor(
            out=c_deviations[0:BATCH],
            in0=c_sums[0:BATCH, 0:1],
            scalar=c_neg_mean[0:BATCH],
            in1=c_sums[0:BATCH, 1:2],
            op0=ALU.mult,
            op1=ALU.add,
        )
        c_variance = small.tile([P, 1], F32)
        nc.vector.tensor_scalar(
            out=c_variance[0:BATCH],
            in0=c_deviations[0:BATCH],
            scalar1=1.0 / (WIDTH - 1),
            scalar2=0.0,
            op0=ALU.mult,
            op1=ALU.max,
        )
        c_std = square_root(c_variance, BATCH)
        c_inv_std = inverse(c_std, BATCH)
        c_shift = small.tile([P, 1], F32)
        nc.vector.tensor_tensor(
            out=c_shift[0:BATCH], in0=c_neg_mean[0:BATCH], in1=c_inv_std[0:BATCH], op=ALU.mult
        )
        c_normal = small.tile([P, WIDTH], F32)
        nc.scalar.activation(
            out=c_normal[0:BATCH],
            in_=c_copy[0:BATCH],
            func=ACT.Identity,
            scale=c_inv_std[0:BATCH],
            bias=c_shift[0:BATCH],
        )
        c_scaled = small.tile([P, WIDTH], F32)
        nc.vector.tensor_tensor(
            out=c_scaled[0:BATCH], in0=c_normal[0:BATCH], in1=gamma_sum[0:BATCH], op=ALU.mult
        )
        c_result = small.tile([P, WIDTH], F32)
        nc.vector.tensor_tensor(
            out=c_result[0:BATCH], in0=c_scaled[0:BATCH], in1=beta_sum_one[0:BATCH], op=ALU.add
        )
        nc.sync.dma_start(out=o_sum[:, :], in_=c_result[0:BATCH])
        second_matmuls((2, 3), y_operand_of[last - 1], z_banks)
        all_row_statistics((2, 3), z_banks, stats)
        moments = row_moments(stats)
        last_z_banks = [ring.tile([P, WIDTH], F32, tag="ring", name="last_z_bank") for i in range(I_TILES)]
        last_stats = small.tile([P, I_TILES, 6], F32, name="stats")
        second_matmul(0, last_z_banks[0], *y_operand_of[last][1:])
        second_matmul(1, last_z_banks[1], *y_operand_of[last][1:])
        total_moments(moments, last_z_banks[3][:, 0:2], averager)
        neg_mean, variance = mean_and_variance(last_z_banks[3][:, 0:2])
        gained = [subtract_mean_and_gain(0, z_banks[0], neg_mean)]
        second_matmul(2, last_z_banks[2], *y_operand_of[last][1:])
        second_matmul(3, last_z_banks[3], *y_operand_of[last][1:])
        all_row_statistics((0, 1), last_z_banks, last_stats)
        last_sums = small.tile([P, 2, 2], F32, name="sums")
        for i in (2, 3):
            scalar_sums(i - 2, last_z_banks[i], last_sums)
        last_moments = joined_moments(last_stats[:, 0:2, :], last_sums)
        std = square_root(variance, P)
        inv_std = inverse(std, P)
        gained.extend([subtract_mean_and_gain(i, z_banks[i], neg_mean) for i in (1, 2, 3)])
        totals = z_pool.tile([P, WIDTH], F32, name="z_bank")
        total_moments(last_moments, totals[:, 0:2], half_averager)
        last_neg_mean, last_variance = mean_and_variance(totals[:, 0:2])
        last_std = square_root(last_variance, P)
        for i in range(I_TILES):
            divide_by_std_and_bias(last - 1, i, gained[i], inv_std)
        last_gained = [subtract_mean_and_gain(i, last_z_banks[i], last_neg_mean) for i in (0, 1)]
        last_inv_std = inverse(last_std, P)
        divide_by_std_and_bias(last, 0, last_gained[0], last_inv_std)
        divide_by_std_and_bias(last, 1, last_gained[1], last_inv_std)
        for i in (2, 3):
            last_gained.append(subtract_mean_and_gain(i, last_z_banks[i], last_neg_mean))
            divide_by_std_and_bias(last, i, last_gained[i], last_inv_std)
